import numpy as np
import ml_dtypes


def mxq(x, axis, fmt="e4m3"):
    dtype, down = {"e4m3": (ml_dtypes.float8_e4m3fn, 7), "e5m2": (ml_dtypes.float8_e5m2, 14)}[fmt]
    v = np.moveaxis(np.asarray(x, np.float32).astype(ml_dtypes.bfloat16).astype(np.float64), axis, -1)
    blocks = v.reshape(v.shape[:-1] + (-1, 32))
    amax = np.abs(blocks).max(-1, keepdims=True)
    byte = np.maximum(np.where(amax > 0, np.frexp(amax)[1] - 1 + 127, 0) - down, 1)
    scale = np.exp2(byte - 127.0)
    codes = (blocks / scale).astype(np.float32).astype(dtype).astype(np.float64)
    return np.moveaxis((codes * scale).reshape(v.shape), -1, axis)


WIDE = False


def mx_kscale(k):
    if not WIDE:
        return np.ones(k)
    levels = np.array([18, -18])
    if k % 512:
        return np.exp2(np.random.permutation(np.resize(levels, k // 32))).repeat(32)
    a = np.empty((k // 512, 16))
    for p in range(k // 512):
        a[p, :8] = np.random.permutation(np.resize(levels, 8))
        for g in range(8):
            far = levels[np.abs(levels - a[p, g]) >= 10]
            a[p, g + 8] = far[np.random.randint(len(far))]
    return np.exp2(a.ravel()).repeat(32)


BF16 = ml_dtypes.bfloat16


def bf(x):
    return np.asarray(x, np.float32).astype(BF16)


def f64(x):
    return np.asarray(x).astype(np.float64)


N, NFEAT, NHEADS, NHID = 1024, 512, 4, 128
C = NHEADS * NHID
P = 0.08


def elu(v):
    return np.where(v > 0, v, np.exp(np.minimum(v, 0.0)) - 1.0)


def setup_inputs():
    s = mx_kscale(N)
    u = mx_kscale(N)
    v = mx_kscale(C)
    edges = np.random.random((N, N)) < P
    x0 = bf(np.random.standard_normal((N, NFEAT)))
    adj0 = bf(edges * (0.5 + np.random.random((N, N))))
    W00 = bf(np.random.standard_normal((NHEADS, NFEAT, NHID)) * 1.5 / np.sqrt(NFEAT * P * N))
    g = bf(np.random.standard_normal((N, C)) * np.exp2(np.random.randint(-6, 1, (N, 1))) * 0.5 * u[:, None] * v)
    p = f64(adj0) @ (f64(x0) @ f64(W00).transpose(1, 0, 2).reshape(NFEAT, C))
    return {"x": bf(f64(x0) * s[:, None]),
            "adj": bf(f64(adj0) / u[:, None] / s),
            "W0": bf(f64(W00) / v.reshape(NHEADS, 1, NHID)),
            "p": np.asarray(p, np.float32),
            "grad_out": g}


def reference(x, adj, W0, p, grad_out):
    dz2 = f64(grad_out) * np.exp(np.minimum(f64(p), 0.0))
    dz1 = mxq(f64(adj), 0, "e4m3").T @ mxq(dz2, 0, "e5m2")
    w = f64(W0).transpose(1, 0, 2).reshape(NFEAT, C)
    dx = mxq(dz1, 1, "e5m2") @ mxq(w, 1, "e4m3").T
    dw = mxq(f64(x), 0, "e4m3").T @ mxq(dz1, 0, "e5m2")
    return dx, dw.reshape(NFEAT, NHEADS, NHID).transpose(1, 0, 2)

@@ -1,0 +1,338 @@
+from contextlib import ExitStack
+
+import concourse.mybir as mybir
+from concourse.masks import make_identity
+
+N, NFEAT, NHEADS, NHID = 1024, 512, 4, 128
+C = NHEADS * NHID
+P = 128
+J = 4
+G = 512
+FLOPS = 2 * N * N * C + 2 * 2 * N * NFEAT * C
+BYTES = 2 * (N * NFEAT + N * N + NFEAT * C + N * C) + 4 * N * C + 4 * (N * NFEAT + NFEAT * C)
+
+F32 = mybir.dt.float32
+BF16 = mybir.dt.bfloat16
+U32 = mybir.dt.uint32
+U8 = mybir.dt.uint8
+E4 = mybir.dt.float8_e4m3fn_x4
+E5 = mybir.dt.float8_e5m2_x4
+ACT = mybir.ActivationFunctionType
+ALU = mybir.AluOpType
+
+def tile_gat_pa_v_kernel(tc, x, adj, W0, p, grad_out, out_0, out_1):
+    nc = tc.nc
+    with ExitStack() as ctx:
+        sb = ctx.enter_context(tc.tile_pool(name="sb", bufs=1))
+        ps = ctx.enter_context(tc.psum_pool(name="ps", bufs=1))
+
+        def st(shape, dtype, name):
+            return sb.tile(shape, dtype, name=name, tag=name, align_bytes=256)
+
+        def bank(i, shape, name):
+            return ps.tile(shape, F32, name=name, tag="b%d" % i)
+
+        adj_raw0 = st([P, J, N], BF16, "ar0")
+        adj_raw1 = [st([P, J, G], BF16, "ar1%d" % g) for g in range(2)]
+        adj_raw = {(0, 0): adj_raw0[:, :, :G], (0, 1): adj_raw0[:, :, G:], (1, 0): adj_raw1[0][:], (1, 1): adj_raw1[1][:]}
+        adj_grp = {(k, g): st([P, G, J], BF16, "ag%d%d" % (k, g)) for k in range(2) for g in range(2)}
+        adj_c = {(k, g): st([P, G], U32, "ac%d%d" % (k, g)) for k in range(2) for g in range(2)}
+        adj_s = {(k, g): st([P, G], U8, "as%d%d" % (k, g)) for k in range(2) for g in range(2)}
+        p_raw = [st([P, J, C], F32, "pr%d" % k) for k in range(2)]
+        e_grp = {(k, h): st([P, C // 2, J], F32, "eg%d%d" % (k, h)) for k in range(2) for h in range(2)}
+        g_raw = [st([P, J, C], BF16, "gr%d" % k) for k in range(2)]
+        dz2 = [st([P, C, J], BF16, "dz%d" % k) for k in range(2)]
+        dz2_c = [st([P, C], U32, "dc%d" % k) for k in range(2)]
+        dz2_s = [st([P, C], U8, "ds%d" % k) for k in range(2)]
+        x_raw = [st([P, J, NFEAT], BF16, "xr%d" % k) for k in range(2)]
+        x_grp = [st([P, NFEAT, J], BF16, "xg%d" % k) for k in range(2)]
+        x_c = [st([P, NFEAT], U32, "xc%d" % k) for k in range(2)]
+        x_s = [st([P, NFEAT], U8, "xs%d" % k) for k in range(2)]
+        w_raw = st([P, NHEADS, 4 * NHID], BF16, "wr")
+        w_srt = st([P, 4, 2, P], F32, "wsrt")
+        w_grp = st([P, NFEAT, J], BF16, "wg")
+        w_c = st([P, NFEAT], U32, "wc")
+        w_s = st([P, NFEAT], U8, "ws")
+        dz1 = [st([P, J, C], BF16, "d1%d" % g) for g in range(2)]
+        nd_grp = [st([P, C, J], BF16, "ng%d" % g) for g in range(2)]
+        nd_c = [st([P, C], U32, "nc%d" % g) for g in range(2)]
+        nd_s = [st([P, C], U8, "ns%d" % g) for g in range(2)]
+        ft_grp = [st([P, G, J], BF16, "fg%d" % g) for g in range(2)]
+        ft_c = [st([P, G], U32, "fc%d" % g) for g in range(2)]
+        ft_s = [st([P, G], U8, "fs%d" % g) for g in range(2)]
+        dx = [st([P, J, NFEAT], F32, "dx%d" % g) for g in range(2)]
+        dw = [st([P, NHEADS, 2, NHID], F32, "dw%d" % i) for i in range(2)]
+        ident = st([P, P], F32, "ident")
+        warm = st([P, 1], F32, "warm")
+
+        def load_adj0():
+            nc.sync.dma_start(out=adj_raw0[:], in_=adj[:G, :].rearrange("(p j) w -> p j w", j=J))
+
+        def load_adj1(g):
+            nc.sync.dma_start(
+                out=adj_raw1[g][:], in_=adj[G:, G * g : G * (g + 1)].rearrange("(p j) w -> p j w", j=J)
+            )
+
+        def load_p(k):
+            nc.sync.dma_start(out=p_raw[k][:], in_=p[G * k : G * (k + 1), :].rearrange("(p j) w -> p j w", j=J))
+
+        def load_g(k):
+            nc.sync.dma_start(out=g_raw[k][:], in_=grad_out[G * k : G * (k + 1), :].rearrange("(p j) w -> p j w", j=J))
+
+        def load_x(k):
+            nc.sync.dma_start(out=x_raw[k][:], in_=x[G * k : G * (k + 1), :].rearrange("(p j) w -> p j w", j=J))
+
+        def load_w():
+            nc.sync.dma_start(out=w_raw[:], in_=W0.rearrange("h (p b) f -> p h (b f)", b=4))
+
+        def exp_p(k, h):
+            nc.scalar.activation(
+                out=e_grp[k, h][:].rearrange("p (c i) t -> p c t i", i=4),
+                in_=p_raw[k][:, :, 256 * h : 256 * (h + 1)].rearrange("p t (c i) -> p c t i", i=4),
+                func=ACT.Exp,
+            )
+
+        def mul(k, h):
+            c = slice(256 * h, 256 * (h + 1))
+            nc.vector.scalar_tensor_tensor(
+                out=dz2[k][:, c, :],
+                in0=e_grp[k, h][:],
+                scalar=1.0,
+                in1=g_raw[k][:, :, c].rearrange("p t c -> p c t"),
+                op0=ALU.min,
+                op1=ALU.mult,
+            )
+
+        def copy(engine, out, in_):
+            if engine == "v":
+                nc.vector.tensor_copy(out=out, in_=in_)
+            else:
+                nc.scalar.copy(out=out, in_=in_)
+
+        def il_adj(k, g, engine, t0, t1):
+            copy(
+                engine,
+                adj_grp[k, g][:].rearrange("p (t m) j -> p m j t", t=J)[:, :, :, t0:t1],
+                adj_raw[k, g].rearrange("p j (m t) -> p m j t", t=J)[:, :, :, t0:t1],
+            )
+
+        def il(grp, raw, engine, c=slice(0, 512)):
+            copy(
+                engine,
+                grp[:, c, :].rearrange("p (c i) t -> p c t i", i=4),
+                raw[:, :, c].rearrange("p t (c i) -> p c t i", i=4),
+            )
+
+        def il_x(k, engine, m):
+            copy(
+                engine,
+                x_grp[k][:].rearrange("p (t m) j -> p m j t", t=J)[:, m],
+                x_raw[k][:].rearrange("p j (m t) -> p m j t", t=J)[:, m],
+            )
+
+        def sort_w(engine):
+            copy(
+                engine,
+                w_srt[:].rearrange("p b u (h q) -> p b h q u", h=NHEADS),
+                w_raw[:].rearrange("p h w -> p (h w)").bitcast(F32).rearrange("p (h b q u) -> p b h q u", h=NHEADS, b=4, u=2),
+            )
+
+        def quant(codes, scales, grp, fmt):
+            nc.vector.quantize_mx(out=codes[:].bitcast(fmt), scales=scales[:], in_=grp[:].rearrange("p c j -> p (c j)"))
+
+        acc = {}
+
+        def mm_dz1(k, g, banks=None):
+            for t in range(J):
+                if k == 0:
+                    acc[g, t] = bank(banks[t], [P, C], "acc%d%d" % (g, t))
+                m = slice(P * t, P * (t + 1))
+                nc.tensor.matmul_mx(
+                    out=acc[g, t][:],
+                    lhsT=adj_c[k, g][:, m].bitcast(E4),
+                    lhsT_scale=adj_s[k, g][:, m],
+                    rhs=dz2_c[k][:].bitcast(E5),
+                    rhs_scale=dz2_s[k][:],
+                    start=(k == 0),
+                    stop=(k == 1),
+                )
+
+        def cast(g, t, engine):
+            copy(engine, dz1[g][:, t, :], acc[g, t][:])
+
+        tr = {}
+
+        def trans(key, b, words, blocks):
+            t_ps = bank(b, [P, 2, 2, P], "tr_%s" % key)
+            tr[key] = t_ps
+            for a, blk in enumerate(blocks):
+                for u in range(2):
+                    nc.tensor.transpose(t_ps[:, a, u, :], words(blk, u), ident[:])
+
+        def tr_out(key, grp, half, engine):
+            words = grp[:].rearrange("p c j -> p (c j)").bitcast(F32)
+            copy(
+                engine,
+                words[:, 512 * half : 512 * (half + 1)].rearrange("p (a r u) -> p a r u", a=2, u=2),
+                tr[key][:].rearrange("p a u r -> p a r u"),
+            )
+
+        def dz1_words(g):
+            w = dz1[g][:].rearrange("p t c -> p (t c)").bitcast(F32)
+            return lambda blk, u: w[:, 256 * blk + u : 256 * (blk + 1) : 2]
+
+        def w_words(blk, u):
+            return w_srt[:, blk, u, :]
+
+        def mm_dx(g, t, b):
+            o = bank(b, [P, NFEAT], "dxp%d%d" % (g, t))
+            acc["dx", g, t] = o
+            m = slice(P * t, P * (t + 1))
+            nc.tensor.matmul_mx(
+                out=o[:],
+                lhsT=ft_c[g][:, m].bitcast(E5),
+                lhsT_scale=ft_s[g][:, m],
+                rhs=w_c[:].bitcast(E4),
+                rhs_scale=w_s[:],
+                start=True,
+                stop=True,
+            )
+
+        def dx_out(g, t, engine):
+            copy(
+                engine,
+                dx[g][:, t, :].rearrange("p (q b) -> p q b", b=4),
+                acc["dx", g, t][:].rearrange("p (b q) -> p q b", b=4),
+            )
+
+        def dx_store(g, h):
+            t = slice(2 * h, 2 * h + 2)
+            nc.sync.dma_start(
+                out=out_0[G * g : G * (g + 1), :].rearrange("(m t) w -> m t w", t=J)[:, t, :], in_=dx[g][:, t, :]
+            )
+
+        def mm_dw(k, i, b):
+            if k == 0:
+                acc["dw", i] = bank(b, [P, C], "dwp%d" % i)
+            m = slice(P * i, P * (i + 1))
+            nc.tensor.matmul_mx(
+                out=acc["dw", i][:],
+                lhsT=x_c[k][:, m].bitcast(E4),
+                lhsT_scale=x_s[k][:, m],
+                rhs=nd_c[k][:].bitcast(E5),
+                rhs_scale=nd_s[k][:],
+                start=(k == 0),
+                stop=(k == 1),
+            )
+
+        def dw_out(i, engine):
+            copy(engine, dw[i // 2][:, :, i % 2, :], acc["dw", i][:].rearrange("p (h f) -> p h f", h=NHEADS))
+
+        def dw_store(h):
+            nc.sync.dma_start(
+                out=out_1.rearrange("h (m b) f -> m h b f", b=4)[:, :, 2 * h : 2 * h + 2, :], in_=dw[h][:]
+            )
+
+        with tc.manual_schedule():
+            nc.vector.memset(warm[:], 0.0)
+            nc.scalar.activation(out=warm[:], in_=warm[:], func=ACT.Exp)
+            make_identity(nc, ident[:])
+
+            load_adj0()
+            load_p(0)
+            load_g(0)
+            load_p(1)
+            load_g(1)
+            load_adj1(0)
+            load_adj1(1)
+            load_w()
+            load_x(0)
+            load_x(1)
+
+            il_adj(0, 0, "s", 3, 4)
+            il_adj(0, 1, "s", 2, 4)
+            il_adj(0, 0, "v", 0, 3)
+            il_adj(0, 1, "v", 0, 2)
+            quant(adj_c[0, 0], adj_s[0, 0], adj_grp[0, 0], E4)
+            quant(adj_c[0, 1], adj_s[0, 1], adj_grp[0, 1], E4)
+            exp_p(0, 0)
+            exp_p(0, 1)
+            mul(0, 0)
+            mul(0, 1)
+            exp_p(1, 0)
+            exp_p(1, 1)
+            quant(dz2_c[0], dz2_s[0], dz2[0], E5)
+            mm_dz1(0, 0, (0, 1, 2, 3))
+            mm_dz1(0, 1, (4, 5, 6, 7))
+            mul(1, 0)
+            mul(1, 1)
+            il_adj(1, 0, "s", 1, 4)
+            il_adj(1, 0, "v", 0, 1)
+            quant(dz2_c[1], dz2_s[1], dz2[1], E5)
+            il_adj(1, 1, "s", 1, 4)
+            il_adj(1, 1, "v", 0, 1)
+            quant(adj_c[1, 0], adj_s[1, 0], adj_grp[1, 0], E4)
+            mm_dz1(1, 0)
+            sort_w("v")
+            quant(adj_c[1, 1], adj_s[1, 1], adj_grp[1, 1], E4)
+            cast(0, 0, "s")
+            cast(0, 1, "s")
+            trans("w0", 0, w_words, (0, 1))
+            mm_dz1(1, 1)
+            cast(0, 2, "s")
+            cast(0, 3, "s")
+            il_x(0, "v", slice(64, 128))
+            il_x(1, "v", slice(0, 128))
+            trans("f00", 1, dz1_words(0), (0, 1))
+            trans("f01", 2, dz1_words(0), (2, 3))
+            trans("w1", 3, w_words, (2, 3))
+            tr_out("w0", w_grp, 0, "s")
+            cast(1, 3, "v")
+            tr_out("f00", ft_grp[0], 0, "v")
+            cast(1, 1, "s")
+            cast(1, 2, "s")
+            tr_out("f01", ft_grp[0], 1, "s")
+            tr_out("w1", w_grp, 1, "s")
+            cast(1, 0, "s")
+            trans("f11", 5, dz1_words(1), (2, 3))
+            trans("f10", 6, dz1_words(1), (0, 1))
+            il(nd_grp[0], dz1[0], "v", slice(0, 256))
+            quant(ft_c[0], ft_s[0], ft_grp[0], E5)
+            quant(w_c, w_s, w_grp, E4)
+            for t in range(J):
+                mm_dx(0, t, (0, 1, 7, 4)[t])
+            tr_out("f11", ft_grp[1], 1, "s")
+            tr_out("f10", ft_grp[1], 0, "s")
+            il_x(0, "v", slice(0, 64))
+            il(nd_grp[1], dz1[1], "v", slice(256, 512))
+            il(nd_grp[0], dz1[0], "v", slice(256, 512))
+            quant(ft_c[1], ft_s[1], ft_grp[1], E5)
+            dx_out(0, 0, "s")
+            dx_out(0, 1, "s")
+            dx_store(0, 0)
+            dx_out(0, 2, "s")
+            dx_out(0, 3, "s")
+            dx_store(0, 1)
+            for t in range(J):
+                mm_dx(1, t, (2, 3, 5, 6)[t])
+            quant(nd_c[0], nd_s[0], nd_grp[0], E5)
+            quant(x_c[0], x_s[0], x_grp[0], E4)
+            for i in range(4):
+                mm_dw(0, i, (0, 1, 7, 4)[i])
+            il(nd_grp[1], dz1[1], "v", slice(0, 256))
+            quant(x_c[1], x_s[1], x_grp[1], E4)
+            quant(nd_c[1], nd_s[1], nd_grp[1], E5)
+            dx_out(1, 0, "s")
+            dx_out(1, 1, "s")
+            dx_store(1, 0)
+            dx_out(1, 2, "s")
+            dx_out(1, 3, "s")
+            dx_store(1, 1)
+            for i in (0, 2, 1, 3):
+                mm_dw(1, i, 0)
+            dw_out(0, "v")
+            dw_out(2, "s")
+            dw_out(1, "v")
+            dw_store(0)
+            dw_out(3, "s")
+            dw_store(1)

@@ -32,22 +32,21 @@ def tile_gat_pa_v_kernel(tc, x, adj, W0, p, grad_out, out_0, out_1):
         def bank(i, shape, name):
             return ps.tile(shape, F32, name=name, tag="b%d" % i)
 
-        adj_raw0 = st([P, J, N], BF16, "ar0")
-        adj_raw1 = [st([P, J, G], BF16, "ar1%d" % g) for g in range(2)]
-        adj_raw = {(0, 0): adj_raw0[:, :, :G], (0, 1): adj_raw0[:, :, G:], (1, 0): adj_raw1[0][:], (1, 1): adj_raw1[1][:]}
-        adj_grp = {(k, g): st([P, G, J], BF16, "ag%d%d" % (k, g)) for k in range(2) for g in range(2)}
+        adj_raw = {(k, g): st([P, J, G], BF16, "ar%d%d" % (k, g)) for k in range(2) for g in range(2)}
+        adj_grp = {(k, g): st([P, J, P, J], BF16, "ag%d%d" % (k, g)) for k in range(2) for g in range(2)}
         adj_c = {(k, g): st([P, G], U32, "ac%d%d" % (k, g)) for k in range(2) for g in range(2)}
         adj_s = {(k, g): st([P, G], U8, "as%d%d" % (k, g)) for k in range(2) for g in range(2)}
-        p_raw = [st([P, J, C], F32, "pr%d" % k) for k in range(2)]
-        e_grp = {(k, h): st([P, C // 2, J], F32, "eg%d%d" % (k, h)) for k in range(2) for h in range(2)}
+        p_raw = {(k, u): st([P, 2, C], F32, "pr%d%d" % (k, u)) for k in range(2) for u in range(2)}
+        p_neg = {(k, u, h): st([P, 64, 2, 4], F32, "pn%d%d%d" % (k, u, h)) for k in range(2) for u in range(2) for h in range(2)}
+        e_grp = {(k, h): st([P, 64, J, 4], F32, "eg%d%d" % (k, h)) for k in range(2) for h in range(2)}
         g_raw = [st([P, J, C], BF16, "gr%d" % k) for k in range(2)]
         dz2 = [st([P, C, J], BF16, "dz%d" % k) for k in range(2)]
         dz2_c = [st([P, C], U32, "dc%d" % k) for k in range(2)]
         dz2_s = [st([P, C], U8, "ds%d" % k) for k in range(2)]
         x_raw = [st([P, J, NFEAT], BF16, "xr%d" % k) for k in range(2)]
-        x_grp = [st([P, NFEAT, J], BF16, "xg%d" % k) for k in range(2)]
-        x_c = [st([P, NFEAT], U32, "xc%d" % k) for k in range(2)]
-        x_s = [st([P, NFEAT], U8, "xs%d" % k) for k in range(2)]
+        x_grp = {(k, a): st([P, 2, P, J], BF16, "xg%d%d" % (k, a)) for k in range(2) for a in range(2)}
+        x_c = {(k, a): st([P, 2 * P], U32, "xc%d%d" % (k, a)) for k in range(2) for a in range(2)}
+        x_s = {(k, a): st([P, 2 * P], U8, "xs%d%d" % (k, a)) for k in range(2) for a in range(2)}
         w_raw = st([P, NHEADS, 4 * NHID], BF16, "wr")
         w_srt = st([P, 4, 2, P], F32, "wsrt")
         w_grp = st([P, NFEAT, J], BF16, "wg")
@@ -57,24 +56,23 @@ def tile_gat_pa_v_kernel(tc, x, adj, W0, p, grad_out, out_0, out_1):
         nd_grp = [st([P, C, J], BF16, "ng%d" % g) for g in range(2)]
         nd_c = [st([P, C], U32, "nc%d" % g) for g in range(2)]
         nd_s = [st([P, C], U8, "ns%d" % g) for g in range(2)]
-        ft_grp = [st([P, G, J], BF16, "fg%d" % g) for g in range(2)]
-        ft_c = [st([P, G], U32, "fc%d" % g) for g in range(2)]
-        ft_s = [st([P, G], U8, "fs%d" % g) for g in range(2)]
+        ft_grp = {(g, a): st([P, 2 * P, J], BF16, "fg%d%d" % (g, a)) for g in range(2) for a in range(2)}
+        ft_c = {(g, a): st([P, 2 * P], U32, "fc%d%d" % (g, a)) for g in range(2) for a in range(2)}
+        ft_s = {(g, a): st([P, 2 * P], U8, "fs%d%d" % (g, a)) for g in range(2) for a in range(2)}
         dx = [st([P, J, NFEAT], F32, "dx%d" % g) for g in range(2)]
         dw = [st([P, NHEADS, 2, NHID], F32, "dw%d" % i) for i in range(2)]
         ident = st([P, P], F32, "ident")
         warm = st([P, 1], F32, "warm")
 
-        def load_adj0():
-            nc.sync.dma_start(out=adj_raw0[:], in_=adj[:G, :].rearrange("(p j) w -> p j w", j=J))
-
-        def load_adj1(g):
+        def load_adj(k, g):
             nc.sync.dma_start(
-                out=adj_raw1[g][:], in_=adj[G:, G * g : G * (g + 1)].rearrange("(p j) w -> p j w", j=J)
+                out=adj_raw[k, g][:],
+                in_=adj[G * k : G * (k + 1), G * g : G * (g + 1)].rearrange("(p j) w -> p j w", j=J),
             )
 
-        def load_p(k):
-            nc.sync.dma_start(out=p_raw[k][:], in_=p[G * k : G * (k + 1), :].rearrange("(p j) w -> p j w", j=J))
+        def load_p(k, u):
+            rows = p[G * k : G * (k + 1), :].rearrange("(p j) w -> p j w", j=J)
+            nc.sync.dma_start(out=p_raw[k, u][:], in_=rows[:, 2 * u : 2 * u + 2, :])
 
         def load_g(k):
             nc.sync.dma_start(out=g_raw[k][:], in_=grad_out[G * k : G * (k + 1), :].rearrange("(p j) w -> p j w", j=J))
@@ -85,22 +83,22 @@ def tile_gat_pa_v_kernel(tc, x, adj, W0, p, grad_out, out_0, out_1):
         def load_w():
             nc.sync.dma_start(out=w_raw[:], in_=W0.rearrange("h (p b) f -> p h (b f)", b=4))
 
-        def exp_p(k, h):
-            nc.scalar.activation(
-                out=e_grp[k, h][:].rearrange("p (c i) t -> p c t i", i=4),
-                in_=p_raw[k][:, :, 256 * h : 256 * (h + 1)].rearrange("p t (c i) -> p c t i", i=4),
-                func=ACT.Exp,
-            )
+        def clamp_exp(k, u, h, engine):
+            src = p_raw[k, u][:, :, 256 * h : 256 * (h + 1)].rearrange("p t (c i) -> p c t i", i=4)
+            dst = e_grp[k, h][:, :, 2 * u : 2 * u + 2, :]
+            if engine == "v":
+                nc.vector.tensor_scalar_min(p_neg[k, u, h][:], src, 0.0)
+                return lambda: nc.scalar.activation(out=dst, in_=p_neg[k, u, h][:], func=ACT.Exp)
+            nc.scalar.activation(out=p_neg[k, u, h][:], in_=src, func=ACT.Relu, scale=-1.0)
+            return lambda: nc.scalar.activation(out=dst, in_=p_neg[k, u, h][:], func=ACT.Exp, scale=-1.0)
 
         def mul(k, h):
             c = slice(256 * h, 256 * (h + 1))
-            nc.vector.scalar_tensor_tensor(
-                out=dz2[k][:, c, :],
+            nc.vector.tensor_tensor(
+                out=dz2[k][:, c, :].rearrange("p (c i) t -> p c t i", i=4),
                 in0=e_grp[k, h][:],
-                scalar=1.0,
-                in1=g_raw[k][:, :, c].rearrange("p t c -> p c t"),
-                op0=ALU.min,
-                op1=ALU.mult,
+                in1=g_raw[k][:, :, c].rearrange("p t (c i) -> p c t i", i=4),
+                op=ALU.mult,
             )
 
         def copy(engine, out, in_):
@@ -109,11 +107,11 @@ def tile_gat_pa_v_kernel(tc, x, adj, W0, p, grad_out, out_0, out_1):
             else:
                 nc.scalar.copy(out=out, in_=in_)
 
-        def il_adj(k, g, engine, t0, t1):
+        def il_adj(k, g, engine, m0=0, m1=P, t0=0, t1=J):
             copy(
                 engine,
-                adj_grp[k, g][:].rearrange("p (t m) j -> p m j t", t=J)[:, :, :, t0:t1],
-                adj_raw[k, g].rearrange("p j (m t) -> p m j t", t=J)[:, :, :, t0:t1],
+                adj_grp[k, g][:, t0:t1, m0:m1, :].rearrange("p t m j -> p m j t"),
+                adj_raw[k, g][:].rearrange("p j (m t) -> p m j t", t=J)[:, m0:m1, :, t0:t1],
             )
 
         def il(grp, raw, engine, c=slice(0, 512)):
@@ -123,11 +121,11 @@ def tile_gat_pa_v_kernel(tc, x, adj, W0, p, grad_out, out_0, out_1):
                 raw[:, :, c].rearrange("p t (c i) -> p c t i", i=4),
             )
 
-        def il_x(k, engine, m):
+        def il_x(k, a, engine):
             copy(
                 engine,
-                x_grp[k][:].rearrange("p (t m) j -> p m j t", t=J)[:, m],
-                x_raw[k][:].rearrange("p j (m t) -> p m j t", t=J)[:, m],
+                x_grp[k, a][:].rearrange("p e (m i) j -> p m j i e", i=2),
+                x_raw[k][:, :, 256 * a : 256 * (a + 1)].rearrange("p j (m i e) -> p m j i e", i=2, e=2),
             )
 
         def sort_w(engine):
@@ -138,27 +136,52 @@ def tile_gat_pa_v_kernel(tc, x, adj, W0, p, grad_out, out_0, out_1):
             )
 
         def quant(codes, scales, grp, fmt):
-            nc.vector.quantize_mx(out=codes[:].bitcast(fmt), scales=scales[:], in_=grp[:].rearrange("p c j -> p (c j)"))
+            nc.vector.quantize_mx(out=codes.bitcast(fmt), scales=scales, in_=grp)
+
+        def flat(grp):
+            return grp.rearrange("p c j -> p (c j)")
+
+        def q_adj(k, g, t0=0, t1=J):
+            m = slice(P * t0, P * t1)
+            quant(adj_c[k, g][:, m], adj_s[k, g][:, m], adj_grp[k, g][:, t0:t1].rearrange("p t m j -> p (t m j)"), E4)
+
+        def q_dz2(k, c0=0, c1=C):
+            quant(dz2_c[k][:, c0:c1], dz2_s[k][:, c0:c1], flat(dz2[k][:, c0:c1, :]), E5)
+
+        def q_w():
+            quant(w_c[:], w_s[:], flat(w_grp[:]), E4)
+
+        def q_ft(g, a):
+            quant(ft_c[g, a][:], ft_s[g, a][:], flat(ft_grp[g, a][:]), E5)
+
+        def q_nd(g):
+            quant(nd_c[g][:], nd_s[g][:], flat(nd_grp[g][:]), E5)
+
+        def q_x(k, a):
+            quant(x_c[k, a][:], x_s[k, a][:], x_grp[k, a][:].rearrange("p e m j -> p (e m j)"), E4)
 
         acc = {}
 
-        def mm_dz1(k, g, banks=None):
-            for t in range(J):
-                if k == 0:
-                    acc[g, t] = bank(banks[t], [P, C], "acc%d%d" % (g, t))
-                m = slice(P * t, P * (t + 1))
-                nc.tensor.matmul_mx(
-                    out=acc[g, t][:],
-                    lhsT=adj_c[k, g][:, m].bitcast(E4),
-                    lhsT_scale=adj_s[k, g][:, m],
-                    rhs=dz2_c[k][:].bitcast(E5),
-                    rhs_scale=dz2_s[k][:],
-                    start=(k == 0),
-                    stop=(k == 1),
-                )
+        def mm_dz1(k, g, t, b=None):
+            if k == 0:
+                acc[g, t] = bank(b, [P, C], "acc%d%d" % (g, t))
+            m = slice(P * t, P * (t + 1))
+            nc.tensor.matmul_mx(
+                out=acc[g, t][:],
+                lhsT=adj_c[k, g][:, m].bitcast(E4),
+                lhsT_scale=adj_s[k, g][:, m],
+                rhs=dz2_c[k][:].bitcast(E5),
+                rhs_scale=dz2_s[k][:],
+                start=(k == 0),
+                stop=(k == 1),
+            )
 
         def cast(g, t, engine):
-            copy(engine, dz1[g][:, t, :], acc[g, t][:])
+            copy(
+                engine,
+                dz1[g][:, t, :].rearrange("p (u w e) -> p u w e", u=2, e=2),
+                acc[g, t][:].rearrange("p (w u e) -> p u w e", u=2, e=2),
+            )
 
         tr = {}
 
@@ -169,17 +192,31 @@ def tile_gat_pa_v_kernel(tc, x, adj, W0, p, grad_out, out_0, out_1):
                 for u in range(2):
                     nc.tensor.transpose(t_ps[:, a, u, :], words(blk, u), ident[:])
 
-        def tr_out(key, grp, half, engine):
-            words = grp[:].rearrange("p c j -> p (c j)").bitcast(F32)
+        def tr_out(key, grp, engine):
             copy(
                 engine,
-                words[:, 512 * half : 512 * (half + 1)].rearrange("p (a r u) -> p a r u", a=2, u=2),
+                flat(grp).bitcast(F32).rearrange("p (a r u) -> p a r u", a=2, u=2),
                 tr[key][:].rearrange("p a u r -> p a r u"),
             )
 
         def dz1_words(g):
             w = dz1[g][:].rearrange("p t c -> p (t c)").bitcast(F32)
-            return lambda blk, u: w[:, 256 * blk + u : 256 * (blk + 1) : 2]
+            return lambda blk, u: w[:, 256 * blk + P * u : 256 * blk + P * (u + 1)]
+
+        def tr_ft(g, a, b):
+            trans("f%d%d" % (g, a), b, dz1_words(g), (2 * a, 2 * a + 1))
+
+        def out_ft(g, a, engine):
+            tr_out("f%d%d" % (g, a), ft_grp[g, a][:], engine)
+
+        def tr_w(a, b):
+            trans("w%d" % a, b, w_words, (2 * a, 2 * a + 1))
+
+        def out_w(a, engine):
+            tr_out("w%d" % a, w_grp[:, 256 * a : 256 * (a + 1), :], engine)
+
+        def il_nd(g, h, engine):
+            il(nd_grp[g], dz1[g], engine, slice(256 * h, 256 * (h + 1)))
 
         def w_words(blk, u):
             return w_srt[:, blk, u, :]
@@ -187,11 +224,11 @@ def tile_gat_pa_v_kernel(tc, x, adj, W0, p, grad_out, out_0, out_1):
         def mm_dx(g, t, b):
             o = bank(b, [P, NFEAT], "dxp%d%d" % (g, t))
             acc["dx", g, t] = o
-            m = slice(P * t, P * (t + 1))
+            m = slice(P * (t % 2), P * (t % 2 + 1))
             nc.tensor.matmul_mx(
                 out=o[:],
-                lhsT=ft_c[g][:, m].bitcast(E5),
-                lhsT_scale=ft_s[g][:, m],
+                lhsT=ft_c[g, t // 2][:, m].bitcast(E5),
+                lhsT_scale=ft_s[g, t // 2][:, m],
                 rhs=w_c[:].bitcast(E4),
                 rhs_scale=w_s[:],
                 start=True,
@@ -205,32 +242,37 @@ def tile_gat_pa_v_kernel(tc, x, adj, W0, p, grad_out, out_0, out_1):
                 acc["dx", g, t][:].rearrange("p (b q) -> p q b", b=4),
             )
 
-        def dx_store(g, h):
-            t = slice(2 * h, 2 * h + 2)
+        def dx_store(g, t0, t1):
+            t = slice(t0, t1)
             nc.sync.dma_start(
                 out=out_0[G * g : G * (g + 1), :].rearrange("(m t) w -> m t w", t=J)[:, t, :], in_=dx[g][:, t, :]
             )
 
-        def mm_dw(k, i, b):
+        def mm_dw(k, i, b=None):
             if k == 0:
                 acc["dw", i] = bank(b, [P, C], "dwp%d" % i)
-            m = slice(P * i, P * (i + 1))
+            m = slice(P * (i % 2), P * (i % 2 + 1))
             nc.tensor.matmul_mx(
                 out=acc["dw", i][:],
-                lhsT=x_c[k][:, m].bitcast(E4),
-                lhsT_scale=x_s[k][:, m],
+                lhsT=x_c[k, i // 2][:, m].bitcast(E4),
+                lhsT_scale=x_s[k, i // 2][:, m],
                 rhs=nd_c[k][:].bitcast(E5),
                 rhs_scale=nd_s[k][:],
                 start=(k == 0),
                 stop=(k == 1),
             )
 
-        def dw_out(i, engine):
-            copy(engine, dw[i // 2][:, :, i % 2, :], acc["dw", i][:].rearrange("p (h f) -> p h f", h=NHEADS))
+        def dw_out(i, engine, h0=0, h1=NHEADS):
+            copy(
+                engine,
+                dw[i // 2][:, h0:h1, i % 2, :].rearrange("p h (w u e) -> p h w u e", u=2, e=2),
+                acc["dw", i][:].rearrange("p (u h w e) -> p h w u e", u=2, h=NHEADS, e=2)[:, h0:h1],
+            )
 
-        def dw_store(h):
+        def dw_store(a, h0=0, h1=NHEADS):
             nc.sync.dma_start(
-                out=out_1.rearrange("h (m b) f -> m h b f", b=4)[:, :, 2 * h : 2 * h + 2, :], in_=dw[h][:]
+                out=out_1[h0:h1, 256 * a : 256 * (a + 1), :].rearrange("h (m e) f -> m h e f", e=2),
+                in_=dw[a][:, h0:h1],
             )
 
         with tc.manual_schedule():
@@ -238,101 +280,134 @@ def tile_gat_pa_v_kernel(tc, x, adj, W0, p, grad_out, out_0, out_1):
             nc.scalar.activation(out=warm[:], in_=warm[:], func=ACT.Exp)
             make_identity(nc, ident[:])
 
-            load_adj0()
-            load_p(0)
+            load_p(0, 0)
+            load_p(0, 1)
             load_g(0)
-            load_p(1)
+            load_adj(0, 0)
+            load_p(1, 0)
+            load_p(1, 1)
             load_g(1)
-            load_adj1(0)
-            load_adj1(1)
+            load_adj(1, 0)
             load_w()
+            load_adj(0, 1)
+            load_adj(1, 1)
             load_x(0)
             load_x(1)
 
-            il_adj(0, 0, "s", 3, 4)
-            il_adj(0, 1, "s", 2, 4)
-            il_adj(0, 0, "v", 0, 3)
-            il_adj(0, 1, "v", 0, 2)
-            quant(adj_c[0, 0], adj_s[0, 0], adj_grp[0, 0], E4)
-            quant(adj_c[0, 1], adj_s[0, 1], adj_grp[0, 1], E4)
-            exp_p(0, 0)
-            exp_p(0, 1)
+            for u in range(2):
+                for h in range(2):
+                    clamp_exp(0, u, h, "v")()
             mul(0, 0)
             mul(0, 1)
-            exp_p(1, 0)
-            exp_p(1, 1)
-            quant(dz2_c[0], dz2_s[0], dz2[0], E5)
-            mm_dz1(0, 0, (0, 1, 2, 3))
-            mm_dz1(0, 1, (4, 5, 6, 7))
+            il_adj(0, 0, "s")
+            late = [clamp_exp(1, 0, h, "v") for h in range(2)]
+            q_dz2(0)
+            late[0]()
+            clamp_exp(1, 1, 0, "v")()
+            late[1]()
+            clamp_exp(1, 1, 1, "v")()
+            q_adj(0, 0)
+            for t in range(J):
+                mm_dz1(0, 0, t, t)
             mul(1, 0)
             mul(1, 1)
-            il_adj(1, 0, "s", 1, 4)
-            il_adj(1, 0, "v", 0, 1)
-            quant(dz2_c[1], dz2_s[1], dz2[1], E5)
-            il_adj(1, 1, "s", 1, 4)
-            il_adj(1, 1, "v", 0, 1)
-            quant(adj_c[1, 0], adj_s[1, 0], adj_grp[1, 0], E4)
-            mm_dz1(1, 0)
+            il_adj(1, 0, "s", 0, P, 0, 2)
+            il_adj(1, 0, "s", 0, P, 2, 4)
+            q_dz2(1, 0, 256)
+            q_adj(1, 0, 0, 2)
+            q_dz2(1, 256, 512)
+            mm_dz1(1, 0, 0)
+            mm_dz1(1, 0, 1)
             sort_w("v")
-            quant(adj_c[1, 1], adj_s[1, 1], adj_grp[1, 1], E4)
+            q_adj(1, 0, 2, 4)
+            mm_dz1(1, 0, 2)
+            mm_dz1(1, 0, 3)
+            tr_w(0, 4)
+            tr_w(1, 5)
+            il_adj(0, 1, "v")
             cast(0, 0, "s")
             cast(0, 1, "s")
-            trans("w0", 0, w_words, (0, 1))
-            mm_dz1(1, 1)
+            tr_ft(0, 0, 6)
             cast(0, 2, "s")
             cast(0, 3, "s")
-            il_x(0, "v", slice(64, 128))
-            il_x(1, "v", slice(0, 128))
-            trans("f00", 1, dz1_words(0), (0, 1))
-            trans("f01", 2, dz1_words(0), (2, 3))
-            trans("w1", 3, w_words, (2, 3))
-            tr_out("w0", w_grp, 0, "s")
-            cast(1, 3, "v")
-            tr_out("f00", ft_grp[0], 0, "v")
-            cast(1, 1, "s")
-            cast(1, 2, "s")
-            tr_out("f01", ft_grp[0], 1, "s")
-            tr_out("w1", w_grp, 1, "s")
-            cast(1, 0, "s")
-            trans("f11", 5, dz1_words(1), (2, 3))
-            trans("f10", 6, dz1_words(1), (0, 1))
-            il(nd_grp[0], dz1[0], "v", slice(0, 256))
-            quant(ft_c[0], ft_s[0], ft_grp[0], E5)
-            quant(w_c, w_s, w_grp, E4)
+            tr_ft(0, 1, 7)
+            il_adj(1, 1, "v", 0, P, 0, 2)
+            q_adj(0, 1)
             for t in range(J):
-                mm_dx(0, t, (0, 1, 7, 4)[t])
-            tr_out("f11", ft_grp[1], 1, "s")
-            tr_out("f10", ft_grp[1], 0, "s")
-            il_x(0, "v", slice(0, 64))
-            il(nd_grp[1], dz1[1], "v", slice(256, 512))
-            il(nd_grp[0], dz1[0], "v", slice(256, 512))
-            quant(ft_c[1], ft_s[1], ft_grp[1], E5)
-            dx_out(0, 0, "s")
+                mm_dz1(0, 1, t, t)
+            il_adj(1, 1, "v", 0, P, 2, 4)
+            q_adj(1, 1, 0, 2)
+            mm_dz1(1, 1, 0)
+            mm_dz1(1, 1, 1)
+            out_w(0, "s")
+            out_w(1, "s")
+            il_nd(0, 0, "v")
+            q_adj(1, 1, 2, 4)
+            mm_dz1(1, 1, 2)
+            mm_dz1(1, 1, 3)
+            out_ft(0, 0, "s")
+            q_w()
+            out_ft(0, 1, "s")
+            q_ft(0, 0)
+            mm_dx(0, 0, 4)
+            mm_dx(0, 1, 5)
+            cast(1, 0, "s")
+            cast(1, 1, "s")
+            il_nd(0, 1, "v")
+            q_ft(0, 1)
+            tr_ft(1, 0, 0)
+            mm_dx(0, 2, 6)
+            mm_dx(0, 3, 7)
+            cast(1, 2, "s")
+            cast(1, 3, "s")
+            tr_ft(1, 1, 1)
+            dx_out(0, 0, "v")
+            dx_store(0, 0, 1)
+            out_ft(1, 0, "s")
             dx_out(0, 1, "s")
-            dx_store(0, 0)
+            dx_store(0, 1, 2)
+            out_ft(1, 1, "s")
+            q_nd(0)
+            il_nd(1, 0, "v")
+            q_ft(1, 0)
+            mm_dx(1, 0, 2)
+            mm_dx(1, 1, 3)
+            il_nd(1, 1, "v")
+            q_ft(1, 1)
+            mm_dx(1, 2, 4)
+            mm_dx(1, 3, 5)
             dx_out(0, 2, "s")
             dx_out(0, 3, "s")
-            dx_store(0, 1)
-            for t in range(J):
-                mm_dx(1, t, (2, 3, 5, 6)[t])
-            quant(nd_c[0], nd_s[0], nd_grp[0], E5)
-            quant(x_c[0], x_s[0], x_grp[0], E4)
-            for i in range(4):
-                mm_dw(0, i, (0, 1, 7, 4)[i])
-            il(nd_grp[1], dz1[1], "v", slice(0, 256))
-            quant(x_c[1], x_s[1], x_grp[1], E4)
-            quant(nd_c[1], nd_s[1], nd_grp[1], E5)
+            dx_store(0, 2, 4)
+            il_x(0, 0, "v")
+            q_nd(1)
+            il_x(1, 0, "v")
+            q_x(0, 0)
+            mm_dw(0, 0, 0)
+            mm_dw(0, 1, 1)
+            q_x(1, 0)
+            mm_dw(1, 0)
+            mm_dw(1, 1)
             dx_out(1, 0, "s")
             dx_out(1, 1, "s")
-            dx_store(1, 0)
+            dx_store(1, 0, 2)
+            il_x(0, 1, "v")
+            il_x(1, 1, "v")
+            q_x(0, 1)
+            mm_dw(0, 2, 6)
+            mm_dw(0, 3, 7)
+            q_x(1, 1)
+            mm_dw(1, 2)
+            mm_dw(1, 3)
             dx_out(1, 2, "s")
             dx_out(1, 3, "s")
-            dx_store(1, 1)
-            for i in (0, 2, 1, 3):
-                mm_dw(1, i, 0)
-            dw_out(0, "v")
-            dw_out(2, "s")
+            dx_store(1, 2, 4)
+            dw_out(0, "s")
             dw_out(1, "v")
             dw_store(0)
-            dw_out(3, "s")
-            dw_store(1)
+            dw_out(2, "s", 0, 2)
+            dw_out(3, "v", 0, 2)
+            dw_store(1, 0, 2)
+            dw_out(2, "s", 2, 4)
+            dw_out(3, "v", 2, 4)
+            dw_store(1, 2, 4)

@@ -29,16 +29,16 @@ def tile_gat_pa_v_kernel(tc, x, adj, W0, p, grad_out, out_0, out_1):
         def st(shape, dtype, name):
             return sb.tile(shape, dtype, name=name, tag=name, align_bytes=256)
 
-        def bank(i, shape, name):
-            return ps.tile(shape, F32, name=name, tag="b%d" % i)
+        def bank(i, shape, name, dtype=F32):
+            return ps.tile(shape, dtype, name=name, tag="b%d" % i)
 
         adj_raw = {(k, g): st([P, J, G], BF16, "ar%d%d" % (k, g)) for k in range(2) for g in range(2)}
         adj_grp = {(k, g): st([P, J, P, J], BF16, "ag%d%d" % (k, g)) for k in range(2) for g in range(2)}
         adj_c = {(k, g): st([P, G], U32, "ac%d%d" % (k, g)) for k in range(2) for g in range(2)}
         adj_s = {(k, g): st([P, G], U8, "as%d%d" % (k, g)) for k in range(2) for g in range(2)}
         p_raw = {(k, u): st([P, 2, C], F32, "pr%d%d" % (k, u)) for k in range(2) for u in range(2)}
-        p_neg = {(k, u, h): st([P, 64, 2, 4], F32, "pn%d%d%d" % (k, u, h)) for k in range(2) for u in range(2) for h in range(2)}
-        e_grp = {(k, h): st([P, 64, J, 4], F32, "eg%d%d" % (k, h)) for k in range(2) for h in range(2)}
+        p_neg = {(k, u): st([P, C // 4, 2, 4], F32, "pn%d%d" % (k, u)) for k in range(2) for u in range(2)}
+        e_grp = [st([P, C // 4, J, 4], F32, "eg%d" % k) for k in range(2)]
         g_raw = [st([P, J, C], BF16, "gr%d" % k) for k in range(2)]
         dz2 = [st([P, C, J], BF16, "dz%d" % k) for k in range(2)]
         dz2_c = [st([P, C], U32, "dc%d" % k) for k in range(2)]
@@ -62,6 +62,7 @@ def tile_gat_pa_v_kernel(tc, x, adj, W0, p, grad_out, out_0, out_1):
         dx = [st([P, J, NFEAT], F32, "dx%d" % g) for g in range(2)]
         dw = [st([P, NHEADS, 2, NHID], F32, "dw%d" % i) for i in range(2)]
         ident = st([P, P], F32, "ident")
+        ident_bf = st([P, P], BF16, "identb")
         warm = st([P, 1], F32, "warm")
 
         def load_adj(k, g):
@@ -83,21 +84,22 @@ def tile_gat_pa_v_kernel(tc, x, adj, W0, p, grad_out, out_0, out_1):
         def load_w():
             nc.sync.dma_start(out=w_raw[:], in_=W0.rearrange("h (p b) f -> p h (b f)", b=4))
 
-        def clamp_exp(k, u, h, engine):
-            src = p_raw[k, u][:, :, 256 * h : 256 * (h + 1)].rearrange("p t (c i) -> p c t i", i=4)
-            dst = e_grp[k, h][:, :, 2 * u : 2 * u + 2, :]
-            if engine == "v":
-                nc.vector.tensor_scalar_min(p_neg[k, u, h][:], src, 0.0)
-                return lambda: nc.scalar.activation(out=dst, in_=p_neg[k, u, h][:], func=ACT.Exp)
-            nc.scalar.activation(out=p_neg[k, u, h][:], in_=src, func=ACT.Relu, scale=-1.0)
-            return lambda: nc.scalar.activation(out=dst, in_=p_neg[k, u, h][:], func=ACT.Exp, scale=-1.0)
+        def clamp(k, u, c0, c1):
+            nc.vector.tensor_scalar_min(
+                p_neg[k, u][:, c0 // 4 : c1 // 4],
+                p_raw[k, u][:, :, c0:c1].rearrange("p t (c i) -> p c t i", i=4),
+                0.0,
+            )
 
-        def mul(k, h):
-            c = slice(256 * h, 256 * (h + 1))
+        def exp(k, u, c0, c1):
+            c = slice(c0 // 4, c1 // 4)
+            nc.scalar.activation(out=e_grp[k][:, c, 2 * u : 2 * u + 2, :], in_=p_neg[k, u][:, c], func=ACT.Exp)
+
+        def mul(k, c0, c1):
             nc.vector.tensor_tensor(
-                out=dz2[k][:, c, :].rearrange("p (c i) t -> p c t i", i=4),
-                in0=e_grp[k, h][:],
-                in1=g_raw[k][:, :, c].rearrange("p t (c i) -> p c t i", i=4),
+                out=dz2[k][:, c0:c1, :].rearrange("p (c i) t -> p c t i", i=4),
+                in0=e_grp[k][:, c0 // 4 : c1 // 4],
+                in1=g_raw[k][:, :, c0:c1].rearrange("p t (c i) -> p c t i", i=4),
                 op=ALU.mult,
             )
 
@@ -114,6 +116,27 @@ def tile_gat_pa_v_kernel(tc, x, adj, W0, p, grad_out, out_0, out_1):
                 adj_raw[k, g][:].rearrange("p j (m t) -> p m j t", t=J)[:, m0:m1, :, t0:t1],
             )
 
+        def pe_adj(k, g, a, b):
+            o = bank(b, [P, 2, P, J], "pa%d%d%d" % (k, g, a), BF16)
+            tr["a", k, g, a] = o
+            src = adj_raw[k, g][:].rearrange("p j (m t) -> p j m t", t=J)
+            for h in range(2):
+                m = slice(64 * h, 64 * (h + 1))
+                nc.tensor.matmul(
+                    out=o[:, :, m, :].rearrange("p t m j -> p j m t"),
+                    lhsT=ident_bf[:],
+                    rhs=src[:, :, m, 2 * a : 2 * a + 2],
+                    start=True,
+                    stop=True,
+                )
+
+        def out_adj(k, g, a, engine):
+            copy(
+                engine,
+                adj_grp[k, g][:, 2 * a : 2 * a + 2].rearrange("p t m j -> p (t m j)").bitcast(F32),
+                tr["a", k, g, a][:].rearrange("p t m j -> p (t m j)").bitcast(F32),
+            )
+
         def il(grp, raw, engine, c=slice(0, 512)):
             copy(
                 engine,
@@ -126,6 +149,27 @@ def tile_gat_pa_v_kernel(tc, x, adj, W0, p, grad_out, out_0, out_1):
                 engine,
                 x_grp[k, a][:].rearrange("p e (m i) j -> p m j i e", i=2),
                 x_raw[k][:, :, 256 * a : 256 * (a + 1)].rearrange("p j (m i e) -> p m j i e", i=2, e=2),
+            )
+
+        def pe_x(k, a, b):
+            o = bank(b, [P, 2, P, J], "px%d%d" % (k, a), BF16)
+            tr["x", k, a] = o
+            src = x_raw[k][:, :, 256 * a : 256 * (a + 1)].rearrange("p j (m e) -> p j m e", e=2)
+            for h in range(2):
+                m = slice(64 * h, 64 * (h + 1))
+                nc.tensor.matmul(
+                    out=o[:, :, m, :].rearrange("p e m j -> p j m e"),
+                    lhsT=ident_bf[:],
+                    rhs=src[:, :, m, :],
+                    start=True,
+                    stop=True,
+                )
+
+        def out_x(k, a, engine):
+            copy(
+                engine,
+                x_grp[k, a][:].rearrange("p e m j -> p (e m j)").bitcast(F32),
+                tr["x", k, a][:].rearrange("p e m j -> p (e m j)").bitcast(F32),
             )
 
         def sort_w(engine):
@@ -161,6 +205,7 @@ def tile_gat_pa_v_kernel(tc, x, adj, W0, p, grad_out, out_0, out_1):
             quant(x_c[k, a][:], x_s[k, a][:], x_grp[k, a][:].rearrange("p e m j -> p (e m j)"), E4)
 
         acc = {}
+        tr = {}
 
         def mm_dz1(k, g, t, b=None):
             if k == 0:
@@ -182,8 +227,6 @@ def tile_gat_pa_v_kernel(tc, x, adj, W0, p, grad_out, out_0, out_1):
                 dz1[g][:, t, :].rearrange("p (u w e) -> p u w e", u=2, e=2),
                 acc[g, t][:].rearrange("p (w u e) -> p u w e", u=2, e=2),
             )
-
-        tr = {}
 
         def trans(key, b, words, blocks):
             t_ps = bank(b, [P, 2, 2, P], "tr_%s" % key)
@@ -279,6 +322,7 @@ def tile_gat_pa_v_kernel(tc, x, adj, W0, p, grad_out, out_0, out_1):
             nc.vector.memset(warm[:], 0.0)
             nc.scalar.activation(out=warm[:], in_=warm[:], func=ACT.Exp)
             make_identity(nc, ident[:])
+            make_identity(nc, ident_bf[:])
 
             load_p(0, 0)
             load_p(0, 1)
@@ -288,63 +332,86 @@ def tile_gat_pa_v_kernel(tc, x, adj, W0, p, grad_out, out_0, out_1):
             load_p(1, 1)
             load_g(1)
             load_adj(1, 0)
-            load_w()
             load_adj(0, 1)
+            load_w()
             load_adj(1, 1)
             load_x(0)
             load_x(1)
 
-            for u in range(2):
-                for h in range(2):
-                    clamp_exp(0, u, h, "v")()
-            mul(0, 0)
-            mul(0, 1)
-            il_adj(0, 0, "s")
-            late = [clamp_exp(1, 0, h, "v") for h in range(2)]
+            clamp(0, 0, 0, 256)
+            exp(0, 0, 0, 256)
+            clamp(0, 0, 256, C)
+            exp(0, 0, 256, C)
+            clamp(0, 1, 0, 128)
+            exp(0, 1, 0, 128)
+            clamp(0, 1, 128, 256)
+            exp(0, 1, 128, 256)
+            clamp(0, 1, 256, C)
+            exp(0, 1, 256, C)
+            mul(0, 0, 128)
+            mul(0, 128, 256)
+            mul(0, 256, C)
+            pe_adj(0, 0, 1, 4)
+            il_adj(0, 0, "s", 0, P, 0, 2)
+            clamp(1, 0, 0, 256)
+            clamp(1, 0, 256, C)
+            out_adj(0, 0, 1, "s")
+            exp(1, 0, 0, 384)
             q_dz2(0)
-            late[0]()
-            clamp_exp(1, 1, 0, "v")()
-            late[1]()
-            clamp_exp(1, 1, 1, "v")()
+            clamp(1, 1, 0, 128)
+            exp(1, 1, 0, 128)
+            clamp(1, 1, 128, 256)
+            exp(1, 1, 128, 256)
+            clamp(1, 1, 256, C)
+            exp(1, 0, 384, C)
+            exp(1, 1, 256, C)
             q_adj(0, 0)
-            for t in range(J):
-                mm_dz1(0, 0, t, t)
-            mul(1, 0)
-            mul(1, 1)
+            mm_dz1(0, 0, 0, 0)
+            mm_dz1(0, 0, 1, 1)
+            mm_dz1(0, 0, 2, 2)
+            mm_dz1(0, 0, 3, 3)
+            mul(1, 0, 128)
+            mul(1, 128, 256)
+            mul(1, 256, C)
             il_adj(1, 0, "s", 0, P, 0, 2)
             il_adj(1, 0, "s", 0, P, 2, 4)
+            pe_adj(0, 1, 0, 6)
             q_dz2(1, 0, 256)
-            q_adj(1, 0, 0, 2)
             q_dz2(1, 256, 512)
+            q_adj(1, 0, 0, 2)
             mm_dz1(1, 0, 0)
             mm_dz1(1, 0, 1)
-            sort_w("v")
+            il_adj(0, 1, "v", 0, P, 2, 4)
+            out_adj(0, 1, 0, "s")
             q_adj(1, 0, 2, 4)
             mm_dz1(1, 0, 2)
             mm_dz1(1, 0, 3)
+            sort_w("v")
             tr_w(0, 4)
             tr_w(1, 5)
-            il_adj(0, 1, "v")
             cast(0, 0, "s")
             cast(0, 1, "s")
+            q_adj(0, 1)
+            mm_dz1(0, 1, 0, 0)
             tr_ft(0, 0, 6)
+            mm_dz1(0, 1, 1, 1)
             cast(0, 2, "s")
             cast(0, 3, "s")
-            tr_ft(0, 1, 7)
             il_adj(1, 1, "v", 0, P, 0, 2)
-            q_adj(0, 1)
-            for t in range(J):
-                mm_dz1(0, 1, t, t)
             il_adj(1, 1, "v", 0, P, 2, 4)
+            mm_dz1(0, 1, 2, 2)
+            tr_ft(0, 1, 7)
+            mm_dz1(0, 1, 3, 3)
             q_adj(1, 1, 0, 2)
             mm_dz1(1, 1, 0)
             mm_dz1(1, 1, 1)
             out_w(0, "s")
             out_w(1, "s")
-            il_nd(0, 0, "v")
             q_adj(1, 1, 2, 4)
             mm_dz1(1, 1, 2)
             mm_dz1(1, 1, 3)
+            il_nd(0, 0, "v")
+            il_x(0, 0, "v")
             out_ft(0, 0, "s")
             q_w()
             out_ft(0, 1, "s")
@@ -361,45 +428,47 @@ def tile_gat_pa_v_kernel(tc, x, adj, W0, p, grad_out, out_0, out_1):
             cast(1, 2, "s")
             cast(1, 3, "s")
             tr_ft(1, 1, 1)
+            q_x(0, 0)
             dx_out(0, 0, "v")
             dx_store(0, 0, 1)
-            out_ft(1, 0, "s")
+            q_nd(0)
+            pe_x(0, 1, 4)
             dx_out(0, 1, "s")
             dx_store(0, 1, 2)
+            out_ft(1, 0, "s")
+            dx_out(0, 2, "s")
+            dx_store(0, 2, 3)
             out_ft(1, 1, "s")
-            q_nd(0)
             il_nd(1, 0, "v")
+            il_x(1, 0, "v")
             q_ft(1, 0)
-            mm_dx(1, 0, 2)
-            mm_dx(1, 1, 3)
+            mm_dx(1, 0, 5)
+            mm_dx(1, 1, 0)
+            mm_dw(0, 0, 2)
+            mm_dw(0, 1, 3)
             il_nd(1, 1, "v")
             q_ft(1, 1)
-            mm_dx(1, 2, 4)
-            mm_dx(1, 3, 5)
-            dx_out(0, 2, "s")
             dx_out(0, 3, "s")
-            dx_store(0, 2, 4)
-            il_x(0, 0, "v")
-            q_nd(1)
-            il_x(1, 0, "v")
-            q_x(0, 0)
-            mm_dw(0, 0, 0)
-            mm_dw(0, 1, 1)
+            dx_store(0, 3, 4)
+            out_x(0, 1, "s")
+            mm_dx(1, 2, 6)
+            mm_dx(1, 3, 1)
             q_x(1, 0)
+            q_nd(1)
             mm_dw(1, 0)
             mm_dw(1, 1)
-            dx_out(1, 0, "s")
-            dx_out(1, 1, "s")
-            dx_store(1, 0, 2)
-            il_x(0, 1, "v")
-            il_x(1, 1, "v")
             q_x(0, 1)
-            mm_dw(0, 2, 6)
-            mm_dw(0, 3, 7)
+            mm_dw(0, 2, 7)
+            mm_dw(0, 3, 4)
+            dx_out(1, 0, "s")
+            dx_store(1, 0, 1)
+            dx_out(1, 1, "s")
+            dx_store(1, 1, 2)
+            il_x(1, 1, "v")
+            dx_out(1, 2, "v")
             q_x(1, 1)
             mm_dw(1, 2)
             mm_dw(1, 3)
-            dx_out(1, 2, "s")
             dx_out(1, 3, "s")
             dx_store(1, 2, 4)
             dw_out(0, "s")

@@ -32,7 +32,9 @@ def tile_gat_pa_v_kernel(tc, x, adj, W0, p, grad_out, out_0, out_1):
         def bank(i, shape, name, dtype=F32):
             return ps.tile(shape, dtype, name=name, tag="b%d" % i)
 
-        adj_raw = {(k, g): st([P, J, G], BF16, "ar%d%d" % (k, g)) for k in range(2) for g in range(2)}
+        adj_top = st([P, J, N], BF16, "ar0")
+        adj_low = [st([P, J, G], BF16, "ar1%d" % g) for g in range(2)]
+        adj_raw = {(0, 0): adj_top[:, :, :G], (0, 1): adj_top[:, :, G:], (1, 0): adj_low[0][:], (1, 1): adj_low[1][:]}
         adj_grp = {(k, g): st([P, J, P, J], BF16, "ag%d%d" % (k, g)) for k in range(2) for g in range(2)}
         adj_c = {(k, g): st([P, G], U32, "ac%d%d" % (k, g)) for k in range(2) for g in range(2)}
         adj_s = {(k, g): st([P, G], U8, "as%d%d" % (k, g)) for k in range(2) for g in range(2)}
@@ -65,10 +67,12 @@ def tile_gat_pa_v_kernel(tc, x, adj, W0, p, grad_out, out_0, out_1):
         ident_bf = st([P, P], BF16, "identb")
         warm = st([P, 1], F32, "warm")
 
-        def load_adj(k, g):
+        def load_adj_top():
+            nc.sync.dma_start(out=adj_top[:], in_=adj[:G, :].rearrange("(p j) w -> p j w", j=J))
+
+        def load_adj_low(g):
             nc.sync.dma_start(
-                out=adj_raw[k, g][:],
-                in_=adj[G * k : G * (k + 1), G * g : G * (g + 1)].rearrange("(p j) w -> p j w", j=J),
+                out=adj_low[g][:], in_=adj[G:, G * g : G * (g + 1)].rearrange("(p j) w -> p j w", j=J)
             )
 
         def load_p(k, u):
@@ -91,9 +95,19 @@ def tile_gat_pa_v_kernel(tc, x, adj, W0, p, grad_out, out_0, out_1):
                 0.0,
             )
 
-        def exp(k, u, c0, c1):
+        def clamp_s(k, u, c0, c1):
+            nc.scalar.activation(
+                out=p_neg[k, u][:, c0 // 4 : c1 // 4],
+                in_=p_raw[k, u][:, :, c0:c1].rearrange("p t (c i) -> p c t i", i=4),
+                func=ACT.Relu,
+                scale=-1.0,
+            )
+
+        def exp(k, u, c0, c1, sign=1.0):
             c = slice(c0 // 4, c1 // 4)
-            nc.scalar.activation(out=e_grp[k][:, c, 2 * u : 2 * u + 2, :], in_=p_neg[k, u][:, c], func=ACT.Exp)
+            nc.scalar.activation(
+                out=e_grp[k][:, c, 2 * u : 2 * u + 2, :], in_=p_neg[k, u][:, c], func=ACT.Exp, scale=sign
+            )
 
         def mul(k, c0, c1):
             nc.vector.tensor_tensor(
@@ -109,17 +123,18 @@ def tile_gat_pa_v_kernel(tc, x, adj, W0, p, grad_out, out_0, out_1):
             else:
                 nc.scalar.copy(out=out, in_=in_)
 
-        def il_adj(k, g, engine, m0=0, m1=P, t0=0, t1=J):
+        def il_adj(k, g, a, engine):
+            t = slice(2 * a, 2 * a + 2)
             copy(
                 engine,
-                adj_grp[k, g][:, t0:t1, m0:m1, :].rearrange("p t m j -> p m j t"),
-                adj_raw[k, g][:].rearrange("p j (m t) -> p m j t", t=J)[:, m0:m1, :, t0:t1],
+                adj_grp[k, g][:, t].rearrange("p t (m i) j -> p m j i t", i=2),
+                adj_raw[k, g].rearrange("p j (m i t) -> p m j i t", i=2, t=J)[:, :, :, :, t],
             )
 
         def pe_adj(k, g, a, b):
             o = bank(b, [P, 2, P, J], "pa%d%d%d" % (k, g, a), BF16)
             tr["a", k, g, a] = o
-            src = adj_raw[k, g][:].rearrange("p j (m t) -> p j m t", t=J)
+            src = adj_raw[k, g].rearrange("p j (m t) -> p j m t", t=J)
             for h in range(2):
                 m = slice(64 * h, 64 * (h + 1))
                 nc.tensor.matmul(
@@ -172,11 +187,11 @@ def tile_gat_pa_v_kernel(tc, x, adj, W0, p, grad_out, out_0, out_1):
                 tr["x", k, a][:].rearrange("p e m j -> p (e m j)").bitcast(F32),
             )
 
-        def sort_w(engine):
+        def sort_w(engine, b0=0, b1=4):
             copy(
                 engine,
-                w_srt[:].rearrange("p b u (h q) -> p b h q u", h=NHEADS),
-                w_raw[:].rearrange("p h w -> p (h w)").bitcast(F32).rearrange("p (h b q u) -> p b h q u", h=NHEADS, b=4, u=2),
+                w_srt[:].rearrange("p b u (h q) -> p b h q u", h=NHEADS)[:, b0:b1],
+                w_raw[:].rearrange("p h w -> p (h w)").bitcast(F32).rearrange("p (h b q u) -> p b h q u", h=NHEADS, b=4, u=2)[:, b0:b1],
             )
 
         def quant(codes, scales, grp, fmt):
@@ -256,7 +271,11 @@ def tile_gat_pa_v_kernel(tc, x, adj, W0, p, grad_out, out_0, out_1):
             trans("w%d" % a, b, w_words, (2 * a, 2 * a + 1))
 
         def out_w(a, engine):
-            tr_out("w%d" % a, w_grp[:, 256 * a : 256 * (a + 1), :], engine)
+            copy(
+                engine,
+                flat(w_grp[:]).bitcast(F32).rearrange("p (r b u) -> p r b u", b=4, u=2)[:, :, 2 * a : 2 * a + 2],
+                tr["w%d" % a][:].rearrange("p b u r -> p r b u"),
+            )
 
         def il_nd(g, h, engine):
             il(nd_grp[g], dz1[g], engine, slice(256 * h, 256 * (h + 1)))
@@ -279,11 +298,7 @@ def tile_gat_pa_v_kernel(tc, x, adj, W0, p, grad_out, out_0, out_1):
             )
 
         def dx_out(g, t, engine):
-            copy(
-                engine,
-                dx[g][:, t, :].rearrange("p (q b) -> p q b", b=4),
-                acc["dx", g, t][:].rearrange("p (b q) -> p q b", b=4),
-            )
+            copy(engine, dx[g][:, t, :], acc["dx", g, t][:])
 
         def dx_store(g, t0, t1):
             t = slice(t0, t1)
@@ -321,156 +336,155 @@ def tile_gat_pa_v_kernel(tc, x, adj, W0, p, grad_out, out_0, out_1):
         with tc.manual_schedule():
             nc.vector.memset(warm[:], 0.0)
             nc.scalar.activation(out=warm[:], in_=warm[:], func=ACT.Exp)
-            make_identity(nc, ident[:])
             make_identity(nc, ident_bf[:])
+            make_identity(nc, ident[:])
 
+            load_adj_top()
             load_p(0, 0)
             load_p(0, 1)
             load_g(0)
-            load_adj(0, 0)
             load_p(1, 0)
             load_p(1, 1)
             load_g(1)
-            load_adj(1, 0)
-            load_adj(0, 1)
+            load_adj_low(0)
             load_w()
-            load_adj(1, 1)
+            load_adj_low(1)
             load_x(0)
             load_x(1)
 
+            pe_adj(0, 0, 1, 4)
+            il_adj(0, 0, 0, "v")
+            il_adj(0, 1, 1, "s")
+            il_adj(0, 1, 0, "v")
             clamp(0, 0, 0, 256)
-            exp(0, 0, 0, 256)
             clamp(0, 0, 256, C)
-            exp(0, 0, 256, C)
+            out_adj(0, 0, 1, "s")
+            exp(0, 0, 0, 256)
+            q_adj(0, 1)
             clamp(0, 1, 0, 128)
             exp(0, 1, 0, 128)
             clamp(0, 1, 128, 256)
             exp(0, 1, 128, 256)
             clamp(0, 1, 256, C)
+            exp(0, 0, 256, C)
             exp(0, 1, 256, C)
+            q_adj(0, 0)
             mul(0, 0, 128)
             mul(0, 128, 256)
             mul(0, 256, C)
-            pe_adj(0, 0, 1, 4)
-            il_adj(0, 0, "s", 0, P, 0, 2)
-            clamp(1, 0, 0, 256)
-            clamp(1, 0, 256, C)
-            out_adj(0, 0, 1, "s")
-            exp(1, 0, 0, 384)
-            q_dz2(0)
+            clamp_s(1, 0, 0, 256)
+            clamp_s(1, 0, 256, 384)
+            exp(1, 0, 0, 256, -1.0)
+            clamp_s(1, 0, 384, C)
             clamp(1, 1, 0, 128)
             exp(1, 1, 0, 128)
             clamp(1, 1, 128, 256)
             exp(1, 1, 128, 256)
             clamp(1, 1, 256, C)
-            exp(1, 0, 384, C)
+            exp(1, 0, 256, C, -1.0)
             exp(1, 1, 256, C)
-            q_adj(0, 0)
-            mm_dz1(0, 0, 0, 0)
-            mm_dz1(0, 0, 1, 1)
-            mm_dz1(0, 0, 2, 2)
-            mm_dz1(0, 0, 3, 3)
+            q_dz2(0)
+            for t in range(J):
+                mm_dz1(0, 0, t, t)
+            mm_dz1(0, 1, 0, 4)
+            mm_dz1(0, 1, 1, 5)
             mul(1, 0, 128)
             mul(1, 128, 256)
             mul(1, 256, C)
-            il_adj(1, 0, "s", 0, P, 0, 2)
-            il_adj(1, 0, "s", 0, P, 2, 4)
-            pe_adj(0, 1, 0, 6)
+            il_adj(1, 0, 0, "s")
+            il_adj(1, 0, 1, "s")
             q_dz2(1, 0, 256)
-            q_dz2(1, 256, 512)
             q_adj(1, 0, 0, 2)
+            q_dz2(1, 256, 512)
             mm_dz1(1, 0, 0)
             mm_dz1(1, 0, 1)
-            il_adj(0, 1, "v", 0, P, 2, 4)
-            out_adj(0, 1, 0, "s")
+            sort_w("v", 0, 2)
+            sort_w("s", 2, 4)
             q_adj(1, 0, 2, 4)
             mm_dz1(1, 0, 2)
             mm_dz1(1, 0, 3)
-            sort_w("v")
-            tr_w(0, 4)
-            tr_w(1, 5)
+            tr_w(0, 6)
+            tr_w(1, 7)
             cast(0, 0, "s")
             cast(0, 1, "s")
-            q_adj(0, 1)
-            mm_dz1(0, 1, 0, 0)
-            tr_ft(0, 0, 6)
-            mm_dz1(0, 1, 1, 1)
-            cast(0, 2, "s")
-            cast(0, 3, "s")
-            il_adj(1, 1, "v", 0, P, 0, 2)
-            il_adj(1, 1, "v", 0, P, 2, 4)
-            mm_dz1(0, 1, 2, 2)
-            tr_ft(0, 1, 7)
-            mm_dz1(0, 1, 3, 3)
+            il_adj(1, 1, 0, "v")
+            il_adj(1, 1, 1, "v")
+            tr_ft(0, 0, 0)
             q_adj(1, 1, 0, 2)
             mm_dz1(1, 1, 0)
             mm_dz1(1, 1, 1)
-            out_w(0, "s")
-            out_w(1, "s")
+            cast(0, 2, "s")
+            cast(0, 3, "s")
             q_adj(1, 1, 2, 4)
+            out_w(0, "v")
+            tr_ft(0, 1, 2)
+            mm_dz1(0, 1, 2, 1)
             mm_dz1(1, 1, 2)
+            mm_dz1(0, 1, 3, 3)
             mm_dz1(1, 1, 3)
-            il_nd(0, 0, "v")
-            il_x(0, 0, "v")
+            out_w(1, "s")
             out_ft(0, 0, "s")
-            q_w()
             out_ft(0, 1, "s")
+            il_x(0, 0, "v")
+            il_nd(0, 0, "v")
+            q_w()
             q_ft(0, 0)
-            mm_dx(0, 0, 4)
-            mm_dx(0, 1, 5)
+            mm_dx(0, 0, 6)
+            mm_dx(0, 1, 7)
+            q_x(0, 0)
+            q_ft(0, 1)
+            mm_dx(0, 2, 0)
+            mm_dx(0, 3, 2)
             cast(1, 0, "s")
             cast(1, 1, "s")
+            tr_ft(1, 0, 4)
             il_nd(0, 1, "v")
-            q_ft(0, 1)
-            tr_ft(1, 0, 0)
-            mm_dx(0, 2, 6)
-            mm_dx(0, 3, 7)
-            cast(1, 2, "s")
-            cast(1, 3, "s")
-            tr_ft(1, 1, 1)
-            q_x(0, 0)
             dx_out(0, 0, "v")
             dx_store(0, 0, 1)
+            cast(1, 2, "s")
+            cast(1, 3, "s")
+            tr_ft(1, 1, 5)
+            pe_x(0, 1, 6)
             q_nd(0)
-            pe_x(0, 1, 4)
+            il_nd(1, 0, "v")
             dx_out(0, 1, "s")
             dx_store(0, 1, 2)
             out_ft(1, 0, "s")
             dx_out(0, 2, "s")
             dx_store(0, 2, 3)
             out_ft(1, 1, "s")
-            il_nd(1, 0, "v")
             il_x(1, 0, "v")
             q_ft(1, 0)
-            mm_dx(1, 0, 5)
-            mm_dx(1, 1, 0)
-            mm_dw(0, 0, 2)
-            mm_dw(0, 1, 3)
+            mm_dx(1, 0, 4)
+            mm_dx(1, 1, 7)
             il_nd(1, 1, "v")
             q_ft(1, 1)
+            mm_dw(0, 0, 1)
+            mm_dw(0, 1, 3)
             dx_out(0, 3, "s")
             dx_store(0, 3, 4)
-            out_x(0, 1, "s")
-            mm_dx(1, 2, 6)
-            mm_dx(1, 3, 1)
+            mm_dx(1, 2, 5)
+            mm_dx(1, 3, 0)
             q_x(1, 0)
             q_nd(1)
             mm_dw(1, 0)
             mm_dw(1, 1)
-            q_x(0, 1)
-            mm_dw(0, 2, 7)
-            mm_dw(0, 3, 4)
             dx_out(1, 0, "s")
             dx_store(1, 0, 1)
             dx_out(1, 1, "s")
             dx_store(1, 1, 2)
             il_x(1, 1, "v")
             dx_out(1, 2, "v")
+            dx_store(1, 2, 3)
+            out_x(0, 1, "s")
+            q_x(0, 1)
+            mm_dw(0, 2, 2)
+            mm_dw(0, 3, 6)
             q_x(1, 1)
             mm_dw(1, 2)
             mm_dw(1, 3)
             dx_out(1, 3, "s")
-            dx_store(1, 2, 4)
+            dx_store(1, 3, 4)
             dw_out(0, "s")
             dw_out(1, "v")
             dw_store(0)

@@ -32,9 +32,7 @@ def tile_gat_pa_v_kernel(tc, x, adj, W0, p, grad_out, out_0, out_1):
         def bank(i, shape, name, dtype=F32):
             return ps.tile(shape, dtype, name=name, tag="b%d" % i)
 
-        adj_top = st([P, J, N], BF16, "ar0")
-        adj_low = [st([P, J, G], BF16, "ar1%d" % g) for g in range(2)]
-        adj_raw = {(0, 0): adj_top[:, :, :G], (0, 1): adj_top[:, :, G:], (1, 0): adj_low[0][:], (1, 1): adj_low[1][:]}
+        adj_raw = {(k, g): st([P, J, G], BF16, "ar%d%d" % (k, g))[:] for k in range(2) for g in range(2)}
         adj_grp = {(k, g): st([P, J, P, J], BF16, "ag%d%d" % (k, g)) for k in range(2) for g in range(2)}
         adj_c = {(k, g): st([P, G], U32, "ac%d%d" % (k, g)) for k in range(2) for g in range(2)}
         adj_s = {(k, g): st([P, G], U8, "as%d%d" % (k, g)) for k in range(2) for g in range(2)}
@@ -46,9 +44,9 @@ def tile_gat_pa_v_kernel(tc, x, adj, W0, p, grad_out, out_0, out_1):
         dz2_c = [st([P, C], U32, "dc%d" % k) for k in range(2)]
         dz2_s = [st([P, C], U8, "ds%d" % k) for k in range(2)]
         x_raw = [st([P, J, NFEAT], BF16, "xr%d" % k) for k in range(2)]
-        x_grp = {(k, a): st([P, 2, P, J], BF16, "xg%d%d" % (k, a)) for k in range(2) for a in range(2)}
-        x_c = {(k, a): st([P, 2 * P], U32, "xc%d%d" % (k, a)) for k in range(2) for a in range(2)}
-        x_s = {(k, a): st([P, 2 * P], U8, "xs%d%d" % (k, a)) for k in range(2) for a in range(2)}
+        x_grp = [st([P, J, P, J], BF16, "xg%d" % k) for k in range(2)]
+        x_c = [st([P, NFEAT], U32, "xc%d" % k) for k in range(2)]
+        x_s = [st([P, NFEAT], U8, "xs%d" % k) for k in range(2)]
         w_raw = st([P, NHEADS, 4 * NHID], BF16, "wr")
         w_srt = st([P, 4, 2, P], F32, "wsrt")
         w_grp = st([P, NFEAT, J], BF16, "wg")
@@ -62,17 +60,14 @@ def tile_gat_pa_v_kernel(tc, x, adj, W0, p, grad_out, out_0, out_1):
         ft_c = {(g, a): st([P, 2 * P], U32, "fc%d%d" % (g, a)) for g in range(2) for a in range(2)}
         ft_s = {(g, a): st([P, 2 * P], U8, "fs%d%d" % (g, a)) for g in range(2) for a in range(2)}
         dx = [st([P, J, NFEAT], F32, "dx%d" % g) for g in range(2)]
-        dw = [st([P, NHEADS, 2, NHID], F32, "dw%d" % i) for i in range(2)]
+        dw = [st([P, J, NHID], F32, "dw%d" % h) for h in range(NHEADS)]
         ident = st([P, P], F32, "ident")
         ident_bf = st([P, P], BF16, "identb")
         warm = st([P, 1], F32, "warm")
 
-        def load_adj_top():
-            nc.sync.dma_start(out=adj_top[:], in_=adj[:G, :].rearrange("(p j) w -> p j w", j=J))
-
-        def load_adj_low(g):
+        def load_adj(k, g):
             nc.sync.dma_start(
-                out=adj_low[g][:], in_=adj[G:, G * g : G * (g + 1)].rearrange("(p j) w -> p j w", j=J)
+                out=adj_raw[k, g], in_=adj[G * k : G * (k + 1), G * g : G * (g + 1)].rearrange("(p j) w -> p j w", j=J)
             )
 
         def load_p(k, u):
@@ -123,13 +118,20 @@ def tile_gat_pa_v_kernel(tc, x, adj, W0, p, grad_out, out_0, out_1):
             else:
                 nc.scalar.copy(out=out, in_=in_)
 
-        def il_adj(k, g, a, engine):
+        def il_sorted(grp, raw, a, engine, m0, m1):
             t = slice(2 * a, 2 * a + 2)
+            m = slice(m0 // 2, m1 // 2)
             copy(
                 engine,
-                adj_grp[k, g][:, t].rearrange("p t (m i) j -> p m j i t", i=2),
-                adj_raw[k, g].rearrange("p j (m i t) -> p m j i t", i=2, t=J)[:, :, :, :, t],
+                grp[:, t].rearrange("p t (m i) j -> p m j i t", i=2)[:, m],
+                raw.rearrange("p j (m i t) -> p m j i t", i=2, t=J)[:, m, :, :, t],
             )
+
+        def il_adj(k, g, a, engine, m0=0, m1=P):
+            il_sorted(adj_grp[k, g], adj_raw[k, g], a, engine, m0, m1)
+
+        def il_x(k, a, engine, m0=0, m1=P):
+            il_sorted(x_grp[k], x_raw[k][:], a, engine, m0, m1)
 
         def pe_adj(k, g, a, b):
             o = bank(b, [P, 2, P, J], "pa%d%d%d" % (k, g, a), BF16)
@@ -150,41 +152,6 @@ def tile_gat_pa_v_kernel(tc, x, adj, W0, p, grad_out, out_0, out_1):
                 engine,
                 adj_grp[k, g][:, 2 * a : 2 * a + 2].rearrange("p t m j -> p (t m j)").bitcast(F32),
                 tr["a", k, g, a][:].rearrange("p t m j -> p (t m j)").bitcast(F32),
-            )
-
-        def il(grp, raw, engine, c=slice(0, 512)):
-            copy(
-                engine,
-                grp[:, c, :].rearrange("p (c i) t -> p c t i", i=4),
-                raw[:, :, c].rearrange("p t (c i) -> p c t i", i=4),
-            )
-
-        def il_x(k, a, engine):
-            copy(
-                engine,
-                x_grp[k, a][:].rearrange("p e (m i) j -> p m j i e", i=2),
-                x_raw[k][:, :, 256 * a : 256 * (a + 1)].rearrange("p j (m i e) -> p m j i e", i=2, e=2),
-            )
-
-        def pe_x(k, a, b):
-            o = bank(b, [P, 2, P, J], "px%d%d" % (k, a), BF16)
-            tr["x", k, a] = o
-            src = x_raw[k][:, :, 256 * a : 256 * (a + 1)].rearrange("p j (m e) -> p j m e", e=2)
-            for h in range(2):
-                m = slice(64 * h, 64 * (h + 1))
-                nc.tensor.matmul(
-                    out=o[:, :, m, :].rearrange("p e m j -> p j m e"),
-                    lhsT=ident_bf[:],
-                    rhs=src[:, :, m, :],
-                    start=True,
-                    stop=True,
-                )
-
-        def out_x(k, a, engine):
-            copy(
-                engine,
-                x_grp[k, a][:].rearrange("p e m j -> p (e m j)").bitcast(F32),
-                tr["x", k, a][:].rearrange("p e m j -> p (e m j)").bitcast(F32),
             )
 
         def sort_w(engine, b0=0, b1=4):
@@ -213,11 +180,13 @@ def tile_gat_pa_v_kernel(tc, x, adj, W0, p, grad_out, out_0, out_1):
         def q_ft(g, a):
             quant(ft_c[g, a][:], ft_s[g, a][:], flat(ft_grp[g, a][:]), E5)
 
-        def q_nd(g):
-            quant(nd_c[g][:], nd_s[g][:], flat(nd_grp[g][:]), E5)
+        def q_nd(g, h0=0, h1=NHEADS):
+            c = slice(NHID * h0, NHID * h1)
+            quant(nd_c[g][:, c], nd_s[g][:, c], flat(nd_grp[g][:, c, :]), E5)
 
-        def q_x(k, a):
-            quant(x_c[k, a][:], x_s[k, a][:], x_grp[k, a][:].rearrange("p e m j -> p (e m j)"), E4)
+        def q_x(k, t0=0, t1=J):
+            m = slice(P * t0, P * t1)
+            quant(x_c[k][:, m], x_s[k][:, m], x_grp[k][:, t0:t1].rearrange("p t m j -> p (t m j)"), E4)
 
         acc = {}
         tr = {}
@@ -236,6 +205,29 @@ def tile_gat_pa_v_kernel(tc, x, adj, W0, p, grad_out, out_0, out_1):
                 stop=(k == 1),
             )
 
+        def mm_quarter(k, q):
+            if k == 0:
+                acc["q", q] = bank(q, [P, J, P], "accq%d" % q)
+            c = slice(P * q, P * (q + 1))
+            for t in range(J):
+                m = slice(P * t, P * (t + 1))
+                nc.tensor.matmul_mx(
+                    out=acc["q", q][:, t, :],
+                    lhsT=adj_c[k, 0][:, m].bitcast(E4),
+                    lhsT_scale=adj_s[k, 0][:, m],
+                    rhs=dz2_c[k][:, c].bitcast(E5),
+                    rhs_scale=dz2_s[k][:, c],
+                    start=(k == 0 and t == 0),
+                    stop=(k == 1 and t == J - 1),
+                )
+
+        def cast_quarter(q, engine):
+            copy(
+                engine,
+                dz1[0][:].rearrange("p t (u w e) -> p t u w e", u=2, e=2)[:, :, :, 32 * q : 32 * (q + 1), :],
+                acc["q", q][:].rearrange("p t (w u e) -> p t u w e", u=2, e=2),
+            )
+
         def cast(g, t, engine):
             copy(
                 engine,
@@ -243,12 +235,12 @@ def tile_gat_pa_v_kernel(tc, x, adj, W0, p, grad_out, out_0, out_1):
                 acc[g, t][:].rearrange("p (w u e) -> p u w e", u=2, e=2),
             )
 
-        def trans(key, b, words, blocks):
-            t_ps = bank(b, [P, 2, 2, P], "tr_%s" % key)
-            tr[key] = t_ps
-            for a, blk in enumerate(blocks):
+        def trans(key, b, words, blocks, first):
+            if b is not None:
+                tr[key] = bank(b, [P, 2, 2, P], "tr_%s" % key)
+            for blk in blocks:
                 for u in range(2):
-                    nc.tensor.transpose(t_ps[:, a, u, :], words(blk, u), ident[:])
+                    nc.tensor.transpose(tr[key][:, blk - first, u, :], words(blk, u), ident[:])
 
         def tr_out(key, grp, engine):
             copy(
@@ -262,13 +254,16 @@ def tile_gat_pa_v_kernel(tc, x, adj, W0, p, grad_out, out_0, out_1):
             return lambda blk, u: w[:, 256 * blk + P * u : 256 * blk + P * (u + 1)]
 
         def tr_ft(g, a, b):
-            trans("f%d%d" % (g, a), b, dz1_words(g), (2 * a, 2 * a + 1))
+            trans("f%d%d" % (g, a), b, dz1_words(g), (2 * a, 2 * a + 1), 2 * a)
+
+        def tr_tile(g, t, b=None):
+            trans("f%d%d" % (g, t // 2), b, dz1_words(g), (t,), t - t % 2)
 
         def out_ft(g, a, engine):
             tr_out("f%d%d" % (g, a), ft_grp[g, a][:], engine)
 
         def tr_w(a, b):
-            trans("w%d" % a, b, w_words, (2 * a, 2 * a + 1))
+            trans("w%d" % a, b, w_words, (2 * a, 2 * a + 1), 2 * a)
 
         def out_w(a, engine):
             copy(
@@ -277,8 +272,19 @@ def tile_gat_pa_v_kernel(tc, x, adj, W0, p, grad_out, out_0, out_1):
                 tr["w%d" % a][:].rearrange("p b u r -> p r b u"),
             )
 
-        def il_nd(g, h, engine):
-            il(nd_grp[g], dz1[g], engine, slice(256 * h, 256 * (h + 1)))
+        def il_nd_half(g, u, engine):
+            copy(
+                engine,
+                nd_grp[g][:].rearrange("p (h u c i) t -> p u h c t i", h=NHEADS, u=2, i=4)[:, u],
+                dz1[g][:].rearrange("p t (u h c i) -> p u h c t i", h=NHEADS, u=2, i=4)[:, u],
+            )
+
+        def il_nd_head(g, h, engine):
+            copy(
+                engine,
+                nd_grp[g][:].rearrange("p (h u c i) t -> p h u c t i", h=NHEADS, u=2, i=4)[:, h],
+                dz1[g][:].rearrange("p t (u h c i) -> p h u c t i", h=NHEADS, u=2, i=4)[:, h],
+            )
 
         def w_words(blk, u):
             return w_srt[:, blk, u, :]
@@ -306,32 +312,31 @@ def tile_gat_pa_v_kernel(tc, x, adj, W0, p, grad_out, out_0, out_1):
                 out=out_0[G * g : G * (g + 1), :].rearrange("(m t) w -> m t w", t=J)[:, t, :], in_=dx[g][:, t, :]
             )
 
-        def mm_dw(k, i, b=None):
+        def mm_dw(k, h, b=None):
             if k == 0:
-                acc["dw", i] = bank(b, [P, C], "dwp%d" % i)
-            m = slice(P * (i % 2), P * (i % 2 + 1))
-            nc.tensor.matmul_mx(
-                out=acc["dw", i][:],
-                lhsT=x_c[k, i // 2][:, m].bitcast(E4),
-                lhsT_scale=x_s[k, i // 2][:, m],
-                rhs=nd_c[k][:].bitcast(E5),
-                rhs_scale=nd_s[k][:],
-                start=(k == 0),
-                stop=(k == 1),
-            )
+                acc["dw", h] = bank(b, [P, J, NHID], "dwp%d" % h)
+            c = slice(NHID * h, NHID * (h + 1))
+            for t in range(J):
+                m = slice(P * t, P * (t + 1))
+                nc.tensor.matmul_mx(
+                    out=acc["dw", h][:, t, :],
+                    lhsT=x_c[k][:, m].bitcast(E4),
+                    lhsT_scale=x_s[k][:, m],
+                    rhs=nd_c[k][:, c].bitcast(E5),
+                    rhs_scale=nd_s[k][:, c],
+                    start=(k == 0 and t == 0),
+                    stop=(k == 1 and t == J - 1),
+                )
 
-        def dw_out(i, engine, h0=0, h1=NHEADS):
+        def dw_out(h, engine):
             copy(
                 engine,
-                dw[i // 2][:, h0:h1, i % 2, :].rearrange("p h (w u e) -> p h w u e", u=2, e=2),
-                acc["dw", i][:].rearrange("p (u h w e) -> p h w u e", u=2, h=NHEADS, e=2)[:, h0:h1],
+                dw[h][:].rearrange("p t (w u e) -> p t w u e", u=2, e=2),
+                acc["dw", h][:].rearrange("p t (u w e) -> p t w u e", u=2, e=2),
             )
 
-        def dw_store(a, h0=0, h1=NHEADS):
-            nc.sync.dma_start(
-                out=out_1[h0:h1, 256 * a : 256 * (a + 1), :].rearrange("h (m e) f -> m h e f", e=2),
-                in_=dw[a][:, h0:h1],
-            )
+        def dw_store(h):
+            nc.sync.dma_start(out=out_1[h].rearrange("(m t) f -> m t f", t=J), in_=dw[h][:])
 
         with tc.manual_schedule():
             nc.vector.memset(warm[:], 0.0)
@@ -339,158 +344,158 @@ def tile_gat_pa_v_kernel(tc, x, adj, W0, p, grad_out, out_0, out_1):
             make_identity(nc, ident_bf[:])
             make_identity(nc, ident[:])
 
-            load_adj_top()
+            load_adj(0, 0)
             load_p(0, 0)
             load_p(0, 1)
             load_g(0)
+            load_adj(1, 0)
             load_p(1, 0)
             load_p(1, 1)
             load_g(1)
-            load_adj_low(0)
             load_w()
-            load_adj_low(1)
+            load_adj(0, 1)
+            load_adj(1, 1)
             load_x(0)
             load_x(1)
 
-            pe_adj(0, 0, 1, 4)
             il_adj(0, 0, 0, "v")
-            il_adj(0, 1, 1, "s")
-            il_adj(0, 1, 0, "v")
+            il_adj(0, 0, 1, "s")
             clamp(0, 0, 0, 256)
             clamp(0, 0, 256, C)
-            out_adj(0, 0, 1, "s")
             exp(0, 0, 0, 256)
-            q_adj(0, 1)
-            clamp(0, 1, 0, 128)
-            exp(0, 1, 0, 128)
-            clamp(0, 1, 128, 256)
-            exp(0, 1, 128, 256)
-            clamp(0, 1, 256, C)
             exp(0, 0, 256, C)
-            exp(0, 1, 256, C)
             q_adj(0, 0)
-            mul(0, 0, 128)
-            mul(0, 128, 256)
-            mul(0, 256, C)
-            clamp_s(1, 0, 0, 256)
-            clamp_s(1, 0, 256, 384)
-            exp(1, 0, 0, 256, -1.0)
-            clamp_s(1, 0, 384, C)
-            clamp(1, 1, 0, 128)
-            exp(1, 1, 0, 128)
-            clamp(1, 1, 128, 256)
-            exp(1, 1, 128, 256)
-            clamp(1, 1, 256, C)
-            exp(1, 0, 256, C, -1.0)
-            exp(1, 1, 256, C)
-            q_dz2(0)
-            for t in range(J):
-                mm_dz1(0, 0, t, t)
-            mm_dz1(0, 1, 0, 4)
-            mm_dz1(0, 1, 1, 5)
-            mul(1, 0, 128)
-            mul(1, 128, 256)
-            mul(1, 256, C)
+            clamp(0, 1, 0, 128)
+            clamp(0, 1, 128, C)
+            for c in range(0, C, 128):
+                exp(0, 1, c, c + 128)
+            for c in range(0, C, 128):
+                mul(0, c, c + 128)
             il_adj(1, 0, 0, "s")
-            il_adj(1, 0, 1, "s")
-            q_dz2(1, 0, 256)
+            il_adj(1, 0, 1, "v")
+            q_dz2(0)
+            for q in range(4):
+                mm_quarter(0, q)
+            clamp_s(1, 0, 0, 256)
+            clamp_s(1, 0, 256, C)
             q_adj(1, 0, 0, 2)
-            q_dz2(1, 256, 512)
-            mm_dz1(1, 0, 0)
-            mm_dz1(1, 0, 1)
-            sort_w("v", 0, 2)
-            sort_w("s", 2, 4)
+            clamp(1, 1, 0, 128)
+            clamp(1, 1, 128, C)
             q_adj(1, 0, 2, 4)
-            mm_dz1(1, 0, 2)
-            mm_dz1(1, 0, 3)
-            tr_w(0, 6)
-            tr_w(1, 7)
-            cast(0, 0, "s")
-            cast(0, 1, "s")
+            exp(1, 0, 0, 256, -1.0)
+            exp(1, 1, 0, 128)
+            exp(1, 1, 128, 256)
+            exp(1, 0, 256, C, -1.0)
+            exp(1, 1, 256, 384)
+            exp(1, 1, 384, C)
+            mul(1, 0, 128)
+            for q in range(4):
+                if q < 3:
+                    mul(1, 128 * (q + 1), 128 * (q + 2))
+                else:
+                    il_adj(0, 1, 0, "v")
+                q_dz2(1, 128 * q, 128 * (q + 1))
+                mm_quarter(1, q)
+                if q == 0:
+                    sort_w("s")
+                if q == 1:
+                    tr_w(0, 4)
+            tr_w(1, 5)
+            cast_quarter(0, "s")
+            cast_quarter(1, "s")
+            out_w(0, "s")
+            cast_quarter(2, "s")
+            cast_quarter(3, "s")
+            il_adj(0, 1, 1, "v")
+            q_adj(0, 1, 0, 2)
+            mm_dz1(0, 1, 0, 0)
+            mm_dz1(0, 1, 1, 1)
+            tr_ft(0, 0, 6)
+            tr_ft(0, 1, 7)
             il_adj(1, 1, 0, "v")
+            q_adj(0, 1, 2, 4)
             il_adj(1, 1, 1, "v")
-            tr_ft(0, 0, 0)
             q_adj(1, 1, 0, 2)
-            mm_dz1(1, 1, 0)
-            mm_dz1(1, 1, 1)
-            cast(0, 2, "s")
-            cast(0, 3, "s")
-            q_adj(1, 1, 2, 4)
-            out_w(0, "v")
-            tr_ft(0, 1, 2)
-            mm_dz1(0, 1, 2, 1)
-            mm_dz1(1, 1, 2)
-            mm_dz1(0, 1, 3, 3)
-            mm_dz1(1, 1, 3)
             out_w(1, "s")
+            il_x(0, 0, "s", 0, 64)
             out_ft(0, 0, "s")
             out_ft(0, 1, "s")
-            il_x(0, 0, "v")
-            il_nd(0, 0, "v")
+            mm_dz1(1, 1, 0)
+            mm_dz1(1, 1, 1)
+            q_adj(1, 1, 2, 4)
+
+            mm_dz1(0, 1, 2, 2)
+            mm_dz1(1, 1, 2)
             q_w()
             q_ft(0, 0)
-            mm_dx(0, 0, 6)
-            mm_dx(0, 1, 7)
-            q_x(0, 0)
+            mm_dx(0, 0, 4)
+            mm_dx(0, 1, 5)
+            il_nd_half(0, 0, "v")
             q_ft(0, 1)
-            mm_dx(0, 2, 0)
-            mm_dx(0, 3, 2)
             cast(1, 0, "s")
             cast(1, 1, "s")
-            tr_ft(1, 0, 4)
-            il_nd(0, 1, "v")
-            dx_out(0, 0, "v")
-            dx_store(0, 0, 1)
-            cast(1, 2, "s")
-            cast(1, 3, "s")
-            tr_ft(1, 1, 5)
-            pe_x(0, 1, 6)
+            mm_dz1(0, 1, 3, 3)
+            tr_ft(1, 0, 0)
+            mm_dz1(1, 1, 3)
+            mm_dx(0, 2, 6)
+            il_nd_half(0, 1, "v")
+            il_x(0, 0, "v", 64, P)
             q_nd(0)
-            il_nd(1, 0, "v")
+            dx_out(0, 0, "s")
+            dx_store(0, 0, 1)
             dx_out(0, 1, "s")
             dx_store(0, 1, 2)
+            cast(1, 2, "s")
+            tr_tile(1, 2, 1)
+            mm_dx(0, 3, 7)
+            cast(1, 3, "s")
+            tr_tile(1, 3)
             out_ft(1, 0, "s")
+            il_x(0, 1, "v")
+            il_x(1, 0, "v")
+            q_x(0)
+            q_ft(1, 0)
+            mm_dw(0, 2, 2)
+            mm_dx(1, 0, 4)
+            mm_dx(1, 1, 5)
+            mm_dw(0, 3, 3)
+            mm_dw(0, 0, 0)
             dx_out(0, 2, "s")
             dx_store(0, 2, 3)
             out_ft(1, 1, "s")
-            il_x(1, 0, "v")
-            q_ft(1, 0)
-            mm_dx(1, 0, 4)
-            mm_dx(1, 1, 7)
-            il_nd(1, 1, "v")
-            q_ft(1, 1)
-            mm_dw(0, 0, 1)
-            mm_dw(0, 1, 3)
             dx_out(0, 3, "s")
             dx_store(0, 3, 4)
-            mm_dx(1, 2, 5)
-            mm_dx(1, 3, 0)
-            q_x(1, 0)
-            q_nd(1)
-            mm_dw(1, 0)
-            mm_dw(1, 1)
+            il_x(1, 1, "v")
+            il_nd_head(1, 0, "v")
+            q_ft(1, 1)
+            q_x(1)
+            mm_dx(1, 2, 6)
+            mm_dw(0, 1, 1)
+            mm_dx(1, 3, 7)
             dx_out(1, 0, "s")
             dx_store(1, 0, 1)
             dx_out(1, 1, "s")
             dx_store(1, 1, 2)
-            il_x(1, 1, "v")
-            dx_out(1, 2, "v")
-            dx_store(1, 2, 3)
-            out_x(0, 1, "s")
-            q_x(0, 1)
-            mm_dw(0, 2, 2)
-            mm_dw(0, 3, 6)
-            q_x(1, 1)
+            il_nd_head(1, 1, "v")
+            q_nd(1, 0, 1)
+            mm_dw(1, 0)
+            il_nd_head(1, 2, "v")
+            q_nd(1, 1, 2)
+            mm_dw(1, 1)
+            il_nd_head(1, 3, "v")
+            q_nd(1, 2, 3)
             mm_dw(1, 2)
-            mm_dw(1, 3)
+            dx_out(1, 2, "s")
+            dx_store(1, 2, 3)
             dx_out(1, 3, "s")
             dx_store(1, 3, 4)
-            dw_out(0, "s")
-            dw_out(1, "v")
+            q_nd(1, 3, 4)
+            mm_dw(1, 3)
+            dw_out(0, "v")
             dw_store(0)
-            dw_out(2, "s", 0, 2)
-            dw_out(3, "v", 0, 2)
-            dw_store(1, 0, 2)
-            dw_out(2, "s", 2, 4)
-            dw_out(3, "v", 2, 4)
-            dw_store(1, 2, 4)
+            dw_out(1, "s")
+            dw_store(1)
+            dw_out(2, "v")
+            dw_store(2)
+            dw_out(3, "s")
+            dw_store(3)

@@ -36,8 +36,8 @@ def tile_gat_pa_v_kernel(tc, x, adj, W0, p, grad_out, out_0, out_1):
         adj_grp = {(k, g): st([P, J, P, J], BF16, "ag%d%d" % (k, g)) for k in range(2) for g in range(2)}
         adj_c = {(k, g): st([P, G], U32, "ac%d%d" % (k, g)) for k in range(2) for g in range(2)}
         adj_s = {(k, g): st([P, G], U8, "as%d%d" % (k, g)) for k in range(2) for g in range(2)}
-        p_raw = {(k, u): st([P, 2, C], F32, "pr%d%d" % (k, u)) for k in range(2) for u in range(2)}
-        p_neg = {(k, u): st([P, C // 4, 2, 4], F32, "pn%d%d" % (k, u)) for k in range(2) for u in range(2)}
+        p_raw = {(k, u): st([P, J, C // 2], F32, "pr%d%d" % (k, u)) for k in range(2) for u in range(2)}
+        p_neg = {(k, u): st([P, C // 8, J, 4], F32, "pn%d%d" % (k, u)) for k in range(2) for u in range(2)}
         e_grp = [st([P, C // 4, J, 4], F32, "eg%d" % k) for k in range(2)]
         g_raw = [st([P, J, C], BF16, "gr%d" % k) for k in range(2)]
         dz2 = [st([P, C, J], BF16, "dz%d" % k) for k in range(2)]
@@ -72,7 +72,7 @@ def tile_gat_pa_v_kernel(tc, x, adj, W0, p, grad_out, out_0, out_1):
 
         def load_p(k, u):
             rows = p[G * k : G * (k + 1), :].rearrange("(p j) w -> p j w", j=J)
-            nc.sync.dma_start(out=p_raw[k, u][:], in_=rows[:, 2 * u : 2 * u + 2, :])
+            nc.sync.dma_start(out=p_raw[k, u][:], in_=rows[:, :, 256 * u : 256 * (u + 1)])
 
         def load_g(k):
             nc.sync.dma_start(out=g_raw[k][:], in_=grad_out[G * k : G * (k + 1), :].rearrange("(p j) w -> p j w", j=J))
@@ -99,9 +99,11 @@ def tile_gat_pa_v_kernel(tc, x, adj, W0, p, grad_out, out_0, out_1):
             )
 
         def exp(k, u, c0, c1, sign=1.0):
-            c = slice(c0 // 4, c1 // 4)
             nc.scalar.activation(
-                out=e_grp[k][:, c, 2 * u : 2 * u + 2, :], in_=p_neg[k, u][:, c], func=ACT.Exp, scale=sign
+                out=e_grp[k][:, 64 * u + c0 // 4 : 64 * u + c1 // 4],
+                in_=p_neg[k, u][:, c0 // 4 : c1 // 4],
+                func=ACT.Exp,
+                scale=sign,
             )
 
         def mul(k, c0, c1):
@@ -360,15 +362,15 @@ def tile_gat_pa_v_kernel(tc, x, adj, W0, p, grad_out, out_0, out_1):
 
             il_adj(0, 0, 0, "v")
             il_adj(0, 0, 1, "s")
-            clamp(0, 0, 0, 256)
-            clamp(0, 0, 256, C)
-            exp(0, 0, 0, 256)
-            exp(0, 0, 256, C)
+            clamp(0, 0, 0, 128)
+            clamp(0, 0, 128, 256)
+            exp(0, 0, 0, 128)
+            exp(0, 0, 128, 256)
             q_adj(0, 0)
             clamp(0, 1, 0, 128)
-            clamp(0, 1, 128, C)
-            for c in range(0, C, 128):
-                exp(0, 1, c, c + 128)
+            clamp(0, 1, 128, 256)
+            exp(0, 1, 0, 128)
+            exp(0, 1, 128, 256)
             for c in range(0, C, 128):
                 mul(0, c, c + 128)
             il_adj(1, 0, 0, "s")
@@ -376,18 +378,16 @@ def tile_gat_pa_v_kernel(tc, x, adj, W0, p, grad_out, out_0, out_1):
             q_dz2(0)
             for q in range(4):
                 mm_quarter(0, q)
-            clamp_s(1, 0, 0, 256)
-            clamp_s(1, 0, 256, C)
+            clamp_s(1, 0, 0, 128)
+            clamp_s(1, 0, 128, 256)
             q_adj(1, 0, 0, 2)
             clamp(1, 1, 0, 128)
-            clamp(1, 1, 128, C)
+            clamp(1, 1, 128, 256)
             q_adj(1, 0, 2, 4)
-            exp(1, 0, 0, 256, -1.0)
+            exp(1, 0, 0, 128, -1.0)
+            exp(1, 0, 128, 256, -1.0)
             exp(1, 1, 0, 128)
             exp(1, 1, 128, 256)
-            exp(1, 0, 256, C, -1.0)
-            exp(1, 1, 256, 384)
-            exp(1, 1, 384, C)
             mul(1, 0, 128)
             for q in range(4):
                 if q < 3:

@@ -63,7 +63,6 @@ def tile_gat_pa_v_kernel(tc, x, adj, W0, p, grad_out, out_0, out_1):
         dw = [st([P, J, NHID], F32, "dw%d" % h) for h in range(NHEADS)]
         ident = st([P, P], F32, "ident")
         ident_bf = st([P, P], BF16, "identb")
-        warm = st([P, 1], F32, "warm")
 
         def load_adj(k, g):
             nc.sync.dma_start(
@@ -341,8 +340,6 @@ def tile_gat_pa_v_kernel(tc, x, adj, W0, p, grad_out, out_0, out_1):
             nc.sync.dma_start(out=out_1[h].rearrange("(m t) f -> m t f", t=J), in_=dw[h][:])
 
         with tc.manual_schedule():
-            nc.vector.memset(warm[:], 0.0)
-            nc.scalar.activation(out=warm[:], in_=warm[:], func=ACT.Exp)
             make_identity(nc, ident_bf[:])
             make_identity(nc, ident[:])
 

@@ -20,6 +20,7 @@ E5 = mybir.dt.float8_e5m2_x4
 ACT = mybir.ActivationFunctionType
 ALU = mybir.AluOpType
 
+
 def tile_gat_pa_v_kernel(tc, x, adj, W0, p, grad_out, out_0, out_1):
     nc = tc.nc
     with ExitStack() as ctx:
@@ -29,8 +30,8 @@ def tile_gat_pa_v_kernel(tc, x, adj, W0, p, grad_out, out_0, out_1):
         def st(shape, dtype, name):
             return sb.tile(shape, dtype, name=name, tag=name, align_bytes=256)
 
-        def bank(i, shape, name, dtype=F32):
-            return ps.tile(shape, dtype, name=name, tag="b%d" % i)
+        def bank(i, shape, name):
+            return ps.tile(shape, F32, name=name, tag="b%d" % i)
 
         adj_raw = {(k, g): st([P, J, G], BF16, "ar%d%d" % (k, g))[:] for k in range(2) for g in range(2)}
         adj_grp = {(k, g): st([P, J, P, J], BF16, "ag%d%d" % (k, g)) for k in range(2) for g in range(2)}
@@ -62,7 +63,6 @@ def tile_gat_pa_v_kernel(tc, x, adj, W0, p, grad_out, out_0, out_1):
         dx = [st([P, J, NFEAT], F32, "dx%d" % g) for g in range(2)]
         dw = [st([P, J, NHID], F32, "dw%d" % h) for h in range(NHEADS)]
         ident = st([P, P], F32, "ident")
-        ident_bf = st([P, P], BF16, "identb")
 
         def load_adj(k, g):
             nc.sync.dma_start(
@@ -89,7 +89,7 @@ def tile_gat_pa_v_kernel(tc, x, adj, W0, p, grad_out, out_0, out_1):
                 0.0,
             )
 
-        def clamp_s(k, u, c0, c1):
+        def clamp_negated(k, u, c0, c1):
             nc.scalar.activation(
                 out=p_neg[k, u][:, c0 // 4 : c1 // 4],
                 in_=p_raw[k, u][:, :, c0:c1].rearrange("p t (c i) -> p c t i", i=4),
@@ -128,38 +128,18 @@ def tile_gat_pa_v_kernel(tc, x, adj, W0, p, grad_out, out_0, out_1):
                 raw.rearrange("p j (m i t) -> p m j i t", i=2, t=J)[:, m, :, :, t],
             )
 
-        def il_adj(k, g, a, engine, m0=0, m1=P):
-            il_sorted(adj_grp[k, g], adj_raw[k, g], a, engine, m0, m1)
+        def il_adj(k, g, a, engine):
+            il_sorted(adj_grp[k, g], adj_raw[k, g], a, engine, 0, P)
 
         def il_x(k, a, engine, m0=0, m1=P):
             il_sorted(x_grp[k], x_raw[k][:], a, engine, m0, m1)
 
-        def pe_adj(k, g, a, b):
-            o = bank(b, [P, 2, P, J], "pa%d%d%d" % (k, g, a), BF16)
-            tr["a", k, g, a] = o
-            src = adj_raw[k, g].rearrange("p j (m t) -> p j m t", t=J)
-            for h in range(2):
-                m = slice(64 * h, 64 * (h + 1))
-                nc.tensor.matmul(
-                    out=o[:, :, m, :].rearrange("p t m j -> p j m t"),
-                    lhsT=ident_bf[:],
-                    rhs=src[:, :, m, 2 * a : 2 * a + 2],
-                    start=True,
-                    stop=True,
-                )
-
-        def out_adj(k, g, a, engine):
+        def sort_w(engine):
+            words = w_raw[:].rearrange("p h w -> p (h w)").bitcast(F32)
             copy(
                 engine,
-                adj_grp[k, g][:, 2 * a : 2 * a + 2].rearrange("p t m j -> p (t m j)").bitcast(F32),
-                tr["a", k, g, a][:].rearrange("p t m j -> p (t m j)").bitcast(F32),
-            )
-
-        def sort_w(engine, b0=0, b1=4):
-            copy(
-                engine,
-                w_srt[:].rearrange("p b u (h q) -> p b h q u", h=NHEADS)[:, b0:b1],
-                w_raw[:].rearrange("p h w -> p (h w)").bitcast(F32).rearrange("p (h b q u) -> p b h q u", h=NHEADS, b=4, u=2)[:, b0:b1],
+                w_srt[:].rearrange("p b u (h q) -> p b h q u", h=NHEADS),
+                words.rearrange("p (h b q u) -> p b h q u", h=NHEADS, b=4, u=2),
             )
 
         def quant(codes, scales, grp, fmt):
@@ -185,9 +165,8 @@ def tile_gat_pa_v_kernel(tc, x, adj, W0, p, grad_out, out_0, out_1):
             c = slice(NHID * h0, NHID * h1)
             quant(nd_c[g][:, c], nd_s[g][:, c], flat(nd_grp[g][:, c, :]), E5)
 
-        def q_x(k, t0=0, t1=J):
-            m = slice(P * t0, P * t1)
-            quant(x_c[k][:, m], x_s[k][:, m], x_grp[k][:, t0:t1].rearrange("p t m j -> p (t m j)"), E4)
+        def q_x(k):
+            quant(x_c[k][:], x_s[k][:], x_grp[k][:].rearrange("p t m j -> p (t m j)"), E4)
 
         acc = {}
         tr = {}
@@ -304,14 +283,10 @@ def tile_gat_pa_v_kernel(tc, x, adj, W0, p, grad_out, out_0, out_1):
                 stop=True,
             )
 
-        def dx_out(g, t, engine):
-            copy(engine, dx[g][:, t, :], acc["dx", g, t][:])
-
-        def dx_store(g, t0, t1):
-            t = slice(t0, t1)
-            nc.sync.dma_start(
-                out=out_0[G * g : G * (g + 1), :].rearrange("(m t) w -> m t w", t=J)[:, t, :], in_=dx[g][:, t, :]
-            )
+        def dx_tile(g, t):
+            copy("s", dx[g][:, t, :], acc["dx", g, t][:])
+            rows = out_0[G * g : G * (g + 1), :].rearrange("(m t) w -> m t w", t=J)
+            nc.sync.dma_start(out=rows[:, t : t + 1, :], in_=dx[g][:, t : t + 1, :])
 
         def mm_dw(k, h, b=None):
             if k == 0:
@@ -329,33 +304,27 @@ def tile_gat_pa_v_kernel(tc, x, adj, W0, p, grad_out, out_0, out_1):
                     stop=(k == 1 and t == J - 1),
                 )
 
-        def dw_out(h, engine):
+        def dw_head(h, engine):
             copy(
                 engine,
                 dw[h][:].rearrange("p t (w u e) -> p t w u e", u=2, e=2),
                 acc["dw", h][:].rearrange("p t (u w e) -> p t w u e", u=2, e=2),
             )
-
-        def dw_store(h):
             nc.sync.dma_start(out=out_1[h].rearrange("(m t) f -> m t f", t=J), in_=dw[h][:])
 
         with tc.manual_schedule():
-            make_identity(nc, ident_bf[:])
             make_identity(nc, ident[:])
 
-            load_adj(0, 0)
-            load_p(0, 0)
-            load_p(0, 1)
-            load_g(0)
-            load_adj(1, 0)
-            load_p(1, 0)
-            load_p(1, 1)
-            load_g(1)
+            for k in range(2):
+                load_adj(k, 0)
+                load_p(k, 0)
+                load_p(k, 1)
+                load_g(k)
             load_w()
-            load_adj(0, 1)
-            load_adj(1, 1)
-            load_x(0)
-            load_x(1)
+            for k in range(2):
+                load_adj(k, 1)
+            for k in range(2):
+                load_x(k)
 
             il_adj(0, 0, 0, "v")
             il_adj(0, 0, 1, "s")
@@ -375,8 +344,9 @@ def tile_gat_pa_v_kernel(tc, x, adj, W0, p, grad_out, out_0, out_1):
             q_dz2(0)
             for q in range(4):
                 mm_quarter(0, q)
-            clamp_s(1, 0, 0, 128)
-            clamp_s(1, 0, 128, 256)
+
+            clamp_negated(1, 0, 0, 128)
+            clamp_negated(1, 0, 128, 256)
             q_adj(1, 0, 0, 2)
             clamp(1, 1, 0, 128)
             clamp(1, 1, 128, 256)
@@ -403,6 +373,7 @@ def tile_gat_pa_v_kernel(tc, x, adj, W0, p, grad_out, out_0, out_1):
             out_w(0, "s")
             cast_quarter(2, "s")
             cast_quarter(3, "s")
+
             il_adj(0, 1, 1, "v")
             q_adj(0, 1, 0, 2)
             mm_dz1(0, 1, 0, 0)
@@ -420,7 +391,6 @@ def tile_gat_pa_v_kernel(tc, x, adj, W0, p, grad_out, out_0, out_1):
             mm_dz1(1, 1, 0)
             mm_dz1(1, 1, 1)
             q_adj(1, 1, 2, 4)
-
             mm_dz1(0, 1, 2, 2)
             mm_dz1(1, 1, 2)
             q_w()
@@ -435,13 +405,12 @@ def tile_gat_pa_v_kernel(tc, x, adj, W0, p, grad_out, out_0, out_1):
             tr_ft(1, 0, 0)
             mm_dz1(1, 1, 3)
             mm_dx(0, 2, 6)
+
             il_nd_half(0, 1, "v")
             il_x(0, 0, "v", 64, P)
             q_nd(0)
-            dx_out(0, 0, "s")
-            dx_store(0, 0, 1)
-            dx_out(0, 1, "s")
-            dx_store(0, 1, 2)
+            dx_tile(0, 0)
+            dx_tile(0, 1)
             cast(1, 2, "s")
             tr_tile(1, 2, 1)
             mm_dx(0, 3, 7)
@@ -457,11 +426,9 @@ def tile_gat_pa_v_kernel(tc, x, adj, W0, p, grad_out, out_0, out_1):
             mm_dx(1, 1, 5)
             mm_dw(0, 3, 3)
             mm_dw(0, 0, 0)
-            dx_out(0, 2, "s")
-            dx_store(0, 2, 3)
+            dx_tile(0, 2)
             out_ft(1, 1, "s")
-            dx_out(0, 3, "s")
-            dx_store(0, 3, 4)
+            dx_tile(0, 3)
             il_x(1, 1, "v")
             il_nd_head(1, 0, "v")
             q_ft(1, 1)
@@ -469,10 +436,9 @@ def tile_gat_pa_v_kernel(tc, x, adj, W0, p, grad_out, out_0, out_1):
             mm_dx(1, 2, 6)
             mm_dw(0, 1, 1)
             mm_dx(1, 3, 7)
-            dx_out(1, 0, "s")
-            dx_store(1, 0, 1)
-            dx_out(1, 1, "s")
-            dx_store(1, 1, 2)
+            dx_tile(1, 0)
+            dx_tile(1, 1)
+
             il_nd_head(1, 1, "v")
             q_nd(1, 0, 1)
             mm_dw(1, 0)
@@ -482,17 +448,9 @@ def tile_gat_pa_v_kernel(tc, x, adj, W0, p, grad_out, out_0, out_1):
             il_nd_head(1, 3, "v")
             q_nd(1, 2, 3)
             mm_dw(1, 2)
-            dx_out(1, 2, "s")
-            dx_store(1, 2, 3)
-            dx_out(1, 3, "s")
-            dx_store(1, 3, 4)
+            dx_tile(1, 2)
+            dx_tile(1, 3)
             q_nd(1, 3, 4)
             mm_dw(1, 3)
-            dw_out(0, "v")
-            dw_store(0)
-            dw_out(1, "s")
-            dw_store(1)
-            dw_out(2, "v")
-            dw_store(2)
-            dw_out(3, "s")
-            dw_store(3)
+            for h in range(NHEADS):
+                dw_head(h, "vs"[h % 2])

from contextlib import ExitStack

import concourse.mybir as mybir
from concourse.masks import make_identity

N, NFEAT, NHEADS, NHID = 1024, 512, 4, 128
C = NHEADS * NHID
P = 128
J = 4
G = 512
FLOPS = 2 * N * N * C + 2 * 2 * N * NFEAT * C
BYTES = 2 * (N * NFEAT + N * N + NFEAT * C + N * C) + 4 * N * C + 4 * (N * NFEAT + NFEAT * C)

F32 = mybir.dt.float32
BF16 = mybir.dt.bfloat16
U32 = mybir.dt.uint32
U8 = mybir.dt.uint8
E4 = mybir.dt.float8_e4m3fn_x4
E5 = mybir.dt.float8_e5m2_x4
ACT = mybir.ActivationFunctionType
ALU = mybir.AluOpType


def tile_gat_pa_v_kernel(tc, x, adj, W0, p, grad_out, out_0, out_1):
    nc = tc.nc
    with ExitStack() as ctx:
        sb = ctx.enter_context(tc.tile_pool(name="sb", bufs=1))
        ps = ctx.enter_context(tc.psum_pool(name="ps", bufs=1))

        def st(shape, dtype, name):
            return sb.tile(shape, dtype, name=name, tag=name, align_bytes=256)

        def bank(i, shape, name):
            return ps.tile(shape, F32, name=name, tag="b%d" % i)

        adj_raw = {(k, g): st([P, J, G], BF16, "ar%d%d" % (k, g))[:] for k in range(2) for g in range(2)}
        adj_grp = {(k, g): st([P, J, P, J], BF16, "ag%d%d" % (k, g)) for k in range(2) for g in range(2)}
        adj_c = {(k, g): st([P, G], U32, "ac%d%d" % (k, g)) for k in range(2) for g in range(2)}
        adj_s = {(k, g): st([P, G], U8, "as%d%d" % (k, g)) for k in range(2) for g in range(2)}
        p_raw = {(k, u): st([P, J, C // 2], F32, "pr%d%d" % (k, u)) for k in range(2) for u in range(2)}
        p_neg = {(k, u): st([P, C // 8, J, 4], F32, "pn%d%d" % (k, u)) for k in range(2) for u in range(2)}
        e_grp = [st([P, C // 4, J, 4], F32, "eg%d" % k) for k in range(2)]
        g_raw = [st([P, J, C], BF16, "gr%d" % k) for k in range(2)]
        dz2 = [st([P, C, J], BF16, "dz%d" % k) for k in range(2)]
        dz2_c = [st([P, C], U32, "dc%d" % k) for k in range(2)]
        dz2_s = [st([P, C], U8, "ds%d" % k) for k in range(2)]
        x_raw = [st([P, J, NFEAT], BF16, "xr%d" % k) for k in range(2)]
        x_grp = [st([P, J, P, J], BF16, "xg%d" % k) for k in range(2)]
        x_c = [st([P, NFEAT], U32, "xc%d" % k) for k in range(2)]
        x_s = [st([P, NFEAT], U8, "xs%d" % k) for k in range(2)]
        w_raw = st([P, NHEADS, 4 * NHID], BF16, "wr")
        w_srt = st([P, 4, 2, P], F32, "wsrt")
        w_grp = st([P, NFEAT, J], BF16, "wg")
        w_c = st([P, NFEAT], U32, "wc")
        w_s = st([P, NFEAT], U8, "ws")
        dz1 = [st([P, J, C], BF16, "d1%d" % g) for g in range(2)]
        nd_grp = [st([P, C, J], BF16, "ng%d" % g) for g in range(2)]
        nd_c = [st([P, C], U32, "nc%d" % g) for g in range(2)]
        nd_s = [st([P, C], U8, "ns%d" % g) for g in range(2)]
        ft_grp = {(g, a): st([P, 2 * P, J], BF16, "fg%d%d" % (g, a)) for g in range(2) for a in range(2)}
        ft_c = {(g, a): st([P, 2 * P], U32, "fc%d%d" % (g, a)) for g in range(2) for a in range(2)}
        ft_s = {(g, a): st([P, 2 * P], U8, "fs%d%d" % (g, a)) for g in range(2) for a in range(2)}
        dx = [st([P, J, NFEAT], F32, "dx%d" % g) for g in range(2)]
        dw = [st([P, J, NHID], F32, "dw%d" % h) for h in range(NHEADS)]
        ident = st([P, P], F32, "ident")

        def load_adj(k, g):
            nc.sync.dma_start(
                out=adj_raw[k, g], in_=adj[G * k : G * (k + 1), G * g : G * (g + 1)].rearrange("(p j) w -> p j w", j=J)
            )

        def load_p(k, u):
            rows = p[G * k : G * (k + 1), :].rearrange("(p j) w -> p j w", j=J)
            nc.sync.dma_start(out=p_raw[k, u][:], in_=rows[:, :, 256 * u : 256 * (u + 1)])

        def load_g(k):
            nc.sync.dma_start(out=g_raw[k][:], in_=grad_out[G * k : G * (k + 1), :].rearrange("(p j) w -> p j w", j=J))

        def load_x(k):
            nc.sync.dma_start(out=x_raw[k][:], in_=x[G * k : G * (k + 1), :].rearrange("(p j) w -> p j w", j=J))

        def load_w():
            nc.sync.dma_start(out=w_raw[:], in_=W0.rearrange("h (p b) f -> p h (b f)", b=4))

        def clamp(k, u, c0, c1):
            nc.vector.tensor_scalar_min(
                p_neg[k, u][:, c0 // 4 : c1 // 4],
                p_raw[k, u][:, :, c0:c1].rearrange("p t (c i) -> p c t i", i=4),
                0.0,
            )

        def clamp_negated(k, u, c0, c1):
            nc.scalar.activation(
                out=p_neg[k, u][:, c0 // 4 : c1 // 4],
                in_=p_raw[k, u][:, :, c0:c1].rearrange("p t (c i) -> p c t i", i=4),
                func=ACT.Relu,
                scale=-1.0,
            )

        def exp(k, u, c0, c1, sign=1.0):
            nc.scalar.activation(
                out=e_grp[k][:, 64 * u + c0 // 4 : 64 * u + c1 // 4],
                in_=p_neg[k, u][:, c0 // 4 : c1 // 4],
                func=ACT.Exp,
                scale=sign,
            )

        def mul(k, c0, c1):
            nc.vector.tensor_tensor(
                out=dz2[k][:, c0:c1, :].rearrange("p (c i) t -> p c t i", i=4),
                in0=e_grp[k][:, c0 // 4 : c1 // 4],
                in1=g_raw[k][:, :, c0:c1].rearrange("p t (c i) -> p c t i", i=4),
                op=ALU.mult,
            )

        def copy(engine, out, in_):
            if engine == "v":
                nc.vector.tensor_copy(out=out, in_=in_)
            else:
                nc.scalar.copy(out=out, in_=in_)

        def il_sorted(grp, raw, a, engine, m0, m1):
            t = slice(2 * a, 2 * a + 2)
            m = slice(m0 // 2, m1 // 2)
            copy(
                engine,
                grp[:, t].rearrange("p t (m i) j -> p m j i t", i=2)[:, m],
                raw.rearrange("p j (m i t) -> p m j i t", i=2, t=J)[:, m, :, :, t],
            )

        def il_adj(k, g, a, engine):
            il_sorted(adj_grp[k, g], adj_raw[k, g], a, engine, 0, P)

        def il_x(k, a, engine, m0=0, m1=P):
            il_sorted(x_grp[k], x_raw[k][:], a, engine, m0, m1)

        def sort_w(engine):
            words = w_raw[:].rearrange("p h w -> p (h w)").bitcast(F32)
            copy(
                engine,
                w_srt[:].rearrange("p b u (h q) -> p b h q u", h=NHEADS),
                words.rearrange("p (h b q u) -> p b h q u", h=NHEADS, b=4, u=2),
            )

        def quant(codes, scales, grp, fmt):
            nc.vector.quantize_mx(out=codes.bitcast(fmt), scales=scales, in_=grp)

        def flat(grp):
            return grp.rearrange("p c j -> p (c j)")

        def q_adj(k, g, t0=0, t1=J):
            m = slice(P * t0, P * t1)
            quant(adj_c[k, g][:, m], adj_s[k, g][:, m], adj_grp[k, g][:, t0:t1].rearrange("p t m j -> p (t m j)"), E4)

        def q_dz2(k, c0=0, c1=C):
            quant(dz2_c[k][:, c0:c1], dz2_s[k][:, c0:c1], flat(dz2[k][:, c0:c1, :]), E5)

        def q_w():
            quant(w_c[:], w_s[:], flat(w_grp[:]), E4)

        def q_ft(g, a):
            quant(ft_c[g, a][:], ft_s[g, a][:], flat(ft_grp[g, a][:]), E5)

        def q_nd(g, h0=0, h1=NHEADS):
            c = slice(NHID * h0, NHID * h1)
            quant(nd_c[g][:, c], nd_s[g][:, c], flat(nd_grp[g][:, c, :]), E5)

        def q_x(k):
            quant(x_c[k][:], x_s[k][:], x_grp[k][:].rearrange("p t m j -> p (t m j)"), E4)

        acc = {}
        tr = {}

        def mm_dz1(k, g, t, b=None):
            if k == 0:
                acc[g, t] = bank(b, [P, C], "acc%d%d" % (g, t))
            m = slice(P * t, P * (t + 1))
            nc.tensor.matmul_mx(
                out=acc[g, t][:],
                lhsT=adj_c[k, g][:, m].bitcast(E4),
                lhsT_scale=adj_s[k, g][:, m],
                rhs=dz2_c[k][:].bitcast(E5),
                rhs_scale=dz2_s[k][:],
                start=(k == 0),
                stop=(k == 1),
            )

        def mm_quarter(k, q):
            if k == 0:
                acc["q", q] = bank(q, [P, J, P], "accq%d" % q)
            c = slice(P * q, P * (q + 1))
            for t in range(J):
                m = slice(P * t, P * (t + 1))
                nc.tensor.matmul_mx(
                    out=acc["q", q][:, t, :],
                    lhsT=adj_c[k, 0][:, m].bitcast(E4),
                    lhsT_scale=adj_s[k, 0][:, m],
                    rhs=dz2_c[k][:, c].bitcast(E5),
                    rhs_scale=dz2_s[k][:, c],
                    start=(k == 0 and t == 0),
                    stop=(k == 1 and t == J - 1),
                )

        def cast_quarter(q, engine):
            copy(
                engine,
                dz1[0][:].rearrange("p t (u w e) -> p t u w e", u=2, e=2)[:, :, :, 32 * q : 32 * (q + 1), :],
                acc["q", q][:].rearrange("p t (w u e) -> p t u w e", u=2, e=2),
            )

        def cast(g, t, engine):
            copy(
                engine,
                dz1[g][:, t, :].rearrange("p (u w e) -> p u w e", u=2, e=2),
                acc[g, t][:].rearrange("p (w u e) -> p u w e", u=2, e=2),
            )

        def trans(key, b, words, blocks, first):
            if b is not None:
                tr[key] = bank(b, [P, 2, 2, P], "tr_%s" % key)
            for blk in blocks:
                for u in range(2):
                    nc.tensor.transpose(tr[key][:, blk - first, u, :], words(blk, u), ident[:])

        def tr_out(key, grp, engine):
            copy(
                engine,
                flat(grp).bitcast(F32).rearrange("p (a r u) -> p a r u", a=2, u=2),
                tr[key][:].rearrange("p a u r -> p a r u"),
            )

        def dz1_words(g):
            w = dz1[g][:].rearrange("p t c -> p (t c)").bitcast(F32)
            return lambda blk, u: w[:, 256 * blk + P * u : 256 * blk + P * (u + 1)]

        def tr_ft(g, a, b):
            trans("f%d%d" % (g, a), b, dz1_words(g), (2 * a, 2 * a + 1), 2 * a)

        def tr_tile(g, t, b=None):
            trans("f%d%d" % (g, t // 2), b, dz1_words(g), (t,), t - t % 2)

        def out_ft(g, a, engine):
            tr_out("f%d%d" % (g, a), ft_grp[g, a][:], engine)

        def tr_w(a, b):
            trans("w%d" % a, b, w_words, (2 * a, 2 * a + 1), 2 * a)

        def out_w(a, engine):
            copy(
                engine,
                flat(w_grp[:]).bitcast(F32).rearrange("p (r b u) -> p r b u", b=4, u=2)[:, :, 2 * a : 2 * a + 2],
                tr["w%d" % a][:].rearrange("p b u r -> p r b u"),
            )

        def il_nd_half(g, u, engine):
            copy(
                engine,
                nd_grp[g][:].rearrange("p (h u c i) t -> p u h c t i", h=NHEADS, u=2, i=4)[:, u],
                dz1[g][:].rearrange("p t (u h c i) -> p u h c t i", h=NHEADS, u=2, i=4)[:, u],
            )

        def il_nd_head(g, h, engine):
            copy(
                engine,
                nd_grp[g][:].rearrange("p (h u c i) t -> p h u c t i", h=NHEADS, u=2, i=4)[:, h],
                dz1[g][:].rearrange("p t (u h c i) -> p h u c t i", h=NHEADS, u=2, i=4)[:, h],
            )

        def w_words(blk, u):
            return w_srt[:, blk, u, :]

        def mm_dx(g, t, b):
            o = bank(b, [P, NFEAT], "dxp%d%d" % (g, t))
            acc["dx", g, t] = o
            m = slice(P * (t % 2), P * (t % 2 + 1))
            nc.tensor.matmul_mx(
                out=o[:],
                lhsT=ft_c[g, t // 2][:, m].bitcast(E5),
                lhsT_scale=ft_s[g, t // 2][:, m],
                rhs=w_c[:].bitcast(E4),
                rhs_scale=w_s[:],
                start=True,
                stop=True,
            )

        def dx_tile(g, t):
            copy("s", dx[g][:, t, :], acc["dx", g, t][:])
            rows = out_0[G * g : G * (g + 1), :].rearrange("(m t) w -> m t w", t=J)
            nc.sync.dma_start(out=rows[:, t : t + 1, :], in_=dx[g][:, t : t + 1, :])

        def mm_dw(k, h, b=None):
            if k == 0:
                acc["dw", h] = bank(b, [P, J, NHID], "dwp%d" % h)
            c = slice(NHID * h, NHID * (h + 1))
            for t in range(J):
                m = slice(P * t, P * (t + 1))
                nc.tensor.matmul_mx(
                    out=acc["dw", h][:, t, :],
                    lhsT=x_c[k][:, m].bitcast(E4),
                    lhsT_scale=x_s[k][:, m],
                    rhs=nd_c[k][:, c].bitcast(E5),
                    rhs_scale=nd_s[k][:, c],
                    start=(k == 0 and t == 0),
                    stop=(k == 1 and t == J - 1),
                )

        def dw_head(h, engine):
            copy(
                engine,
                dw[h][:].rearrange("p t (w u e) -> p t w u e", u=2, e=2),
                acc["dw", h][:].rearrange("p t (u w e) -> p t w u e", u=2, e=2),
            )
            nc.sync.dma_start(out=out_1[h].rearrange("(m t) f -> m t f", t=J), in_=dw[h][:])

        with tc.manual_schedule():
            make_identity(nc, ident[:])

            for k in range(2):
                load_adj(k, 0)
                load_p(k, 0)
                load_p(k, 1)
                load_g(k)
            load_w()
            for k in range(2):
                load_adj(k, 1)
            for k in range(2):
                load_x(k)

            il_adj(0, 0, 0, "v")
            il_adj(0, 0, 1, "s")
            clamp(0, 0, 0, 128)
            clamp(0, 0, 128, 256)
            exp(0, 0, 0, 128)
            exp(0, 0, 128, 256)
            q_adj(0, 0)
            clamp(0, 1, 0, 128)
            clamp(0, 1, 128, 256)
            exp(0, 1, 0, 128)
            exp(0, 1, 128, 256)
            for c in range(0, C, 128):
                mul(0, c, c + 128)
            il_adj(1, 0, 0, "s")
            il_adj(1, 0, 1, "v")
            q_dz2(0)
            for q in range(4):
                mm_quarter(0, q)

            clamp_negated(1, 0, 0, 128)
            clamp_negated(1, 0, 128, 256)
            q_adj(1, 0, 0, 2)
            clamp(1, 1, 0, 128)
            clamp(1, 1, 128, 256)
            q_adj(1, 0, 2, 4)
            exp(1, 0, 0, 128, -1.0)
            exp(1, 0, 128, 256, -1.0)
            exp(1, 1, 0, 128)
            exp(1, 1, 128, 256)
            mul(1, 0, 128)
            for q in range(4):
                if q < 3:
                    mul(1, 128 * (q + 1), 128 * (q + 2))
                else:
                    il_adj(0, 1, 0, "v")
                q_dz2(1, 128 * q, 128 * (q + 1))
                mm_quarter(1, q)
                if q == 0:
                    sort_w("s")
                if q == 1:
                    tr_w(0, 4)
            tr_w(1, 5)
            cast_quarter(0, "s")
            cast_quarter(1, "s")
            out_w(0, "s")
            cast_quarter(2, "s")
            cast_quarter(3, "s")

            il_adj(0, 1, 1, "v")
            q_adj(0, 1, 0, 2)
            mm_dz1(0, 1, 0, 0)
            mm_dz1(0, 1, 1, 1)
            tr_ft(0, 0, 6)
            tr_ft(0, 1, 7)
            il_adj(1, 1, 0, "v")
            q_adj(0, 1, 2, 4)
            il_adj(1, 1, 1, "v")
            q_adj(1, 1, 0, 2)
            out_w(1, "s")
            il_x(0, 0, "s", 0, 64)
            out_ft(0, 0, "s")
            out_ft(0, 1, "s")
            mm_dz1(1, 1, 0)
            mm_dz1(1, 1, 1)
            q_adj(1, 1, 2, 4)
            mm_dz1(0, 1, 2, 2)
            mm_dz1(1, 1, 2)
            q_w()
            q_ft(0, 0)
            mm_dx(0, 0, 4)
            mm_dx(0, 1, 5)
            il_nd_half(0, 0, "v")
            q_ft(0, 1)
            cast(1, 0, "s")
            cast(1, 1, "s")
            mm_dz1(0, 1, 3, 3)
            tr_ft(1, 0, 0)
            mm_dz1(1, 1, 3)
            mm_dx(0, 2, 6)

            il_nd_half(0, 1, "v")
            il_x(0, 0, "v", 64, P)
            q_nd(0)
            dx_tile(0, 0)
            dx_tile(0, 1)
            cast(1, 2, "s")
            tr_tile(1, 2, 1)
            mm_dx(0, 3, 7)
            cast(1, 3, "s")
            tr_tile(1, 3)
            out_ft(1, 0, "s")
            il_x(0, 1, "v")
            il_x(1, 0, "v")
            q_x(0)
            q_ft(1, 0)
            mm_dw(0, 2, 2)
            mm_dx(1, 0, 4)
            mm_dx(1, 1, 5)
            mm_dw(0, 3, 3)
            mm_dw(0, 0, 0)
            dx_tile(0, 2)
            out_ft(1, 1, "s")
            dx_tile(0, 3)
            il_x(1, 1, "v")
            il_nd_head(1, 0, "v")
            q_ft(1, 1)
            q_x(1)
            mm_dx(1, 2, 6)
            mm_dw(0, 1, 1)
            mm_dx(1, 3, 7)
            dx_tile(1, 0)
            dx_tile(1, 1)

            il_nd_head(1, 1, "v")
            q_nd(1, 0, 1)
            mm_dw(1, 0)
            il_nd_head(1, 2, "v")
            q_nd(1, 1, 2)
            mm_dw(1, 1)
            il_nd_head(1, 3, "v")
            q_nd(1, 2, 3)
            mm_dw(1, 2)
            dx_tile(1, 2)
            dx_tile(1, 3)
            q_nd(1, 3, 4)
            mm_dw(1, 3)
            for h in range(NHEADS):
                dw_head(h, "vs"[h % 2])
